import numpy as np
import ml_dtypes


def mxq(x, axis, fmt="e4m3"):
    dtype, down = {"e4m3": (ml_dtypes.float8_e4m3fn, 7), "e5m2": (ml_dtypes.float8_e5m2, 14)}[fmt]
    v = np.moveaxis(np.asarray(x, np.float32).astype(ml_dtypes.bfloat16).astype(np.float64), axis, -1)
    blocks = v.reshape(v.shape[:-1] + (-1, 32))
    amax = np.abs(blocks).max(-1, keepdims=True)
    byte = np.maximum(np.where(amax > 0, np.frexp(amax)[1] - 1 + 127, 0) - down, 1)
    scale = np.exp2(byte - 127.0)
    codes = (blocks / scale).astype(np.float32).astype(dtype).astype(np.float64)
    return np.moveaxis((codes * scale).reshape(v.shape), -1, axis)


WIDE = False


def mx_kscale(k):
    if not WIDE:
        return np.ones(k)
    levels = np.array([10, -10, 5, -5, 0])
    if k % 512:
        return np.exp2(np.random.permutation(np.resize(levels, k // 32))).repeat(32)
    a = np.empty((k // 512, 16))
    for p in range(k // 512):
        a[p, :8] = np.random.permutation(np.resize(levels, 8))
        for g in range(8):
            far = levels[np.abs(levels - a[p, g]) >= 10]
            a[p, g + 8] = far[np.random.randint(len(far))]
    return np.exp2(a.ravel()).repeat(32)


BF16 = ml_dtypes.bfloat16


def bf(x):
    return np.asarray(x, np.float32).astype(BF16)


def f64(x):
    return np.asarray(x).astype(np.float64)


B, T, N, H, G, GH = 32, 4, 8, 512, 9, 3


def sigmoid(v):
    return 1.0 / (1.0 + np.exp(-v))


def draw0():
    s = mx_kscale(H)
    return {"h_new": bf(np.random.standard_normal((B, T, N, H)) * 0.35 * s),
            "c_new": bf(np.random.standard_normal((B, T, N, H)) * 0.8),
            "g_s": bf(np.random.standard_normal((B, T, H)) * s),
            "c_g_s": bf(np.random.standard_normal((B, T, H)) * 0.5),
            "Wg_s": bf(np.random.standard_normal((GH, T, H, H)) * 2.0 / np.sqrt(H) / s[:, None]),
            "Zg_s": bf(np.random.standard_normal((GH, T, H, H)) * 1.0 / np.sqrt(H) / s[:, None]),
            "bg_s": bf(np.random.standard_normal((GH, T, 1, H)) * 0.3)}


def core(h_new, c_new, g_s, c_g_s, Wg_s, Zg_s, bg_s):
    c_new, c_g_s = f64(c_new), f64(c_g_s)
    hq = mxq(f64(h_new).transpose(1, 0, 2, 3).reshape(T, B * N, H), 2, "e4m3")
    preg = (hq @ mxq(f64(Wg_s), 2, "e4m3")) + f64(bg_s)
    preg = preg.reshape(GH, T, B, N, H).transpose(0, 2, 1, 3, 4)
    zs_part = mxq(f64(g_s).transpose(1, 0, 2), 2, "e4m3") @ mxq(f64(Zg_s), 2, "e4m3")
    zs_part = zs_part.transpose(0, 2, 1, 3)[:, :, :, None]
    f_s, gg_s, o_s = sigmoid(preg + zs_part)
    c_g_s_new = np.mean(f_s * c_new, axis=2) + np.mean(gg_s, axis=2) * c_g_s
    g_s_new = np.mean(o_s, axis=2) * np.tanh(c_g_s_new)
    return g_s_new, c_g_s_new


def e4m3fn_bytes(y):
    return np.clip(np.asarray(y, np.float64), -448.0, 448.0).astype(np.float32).astype(ml_dtypes.float8_e4m3fn).view(np.uint8)


def e4m3fn_values(b):
    return np.asarray(b, np.uint8).view(ml_dtypes.float8_e4m3fn).astype(np.float64)


def setup_inputs():
    d = draw0()
    x0 = np.asarray(d['Zg_s']).astype(np.float64)
    s = (np.max(np.abs(x0), axis=(0, 1, 3), keepdims=True) / 448.0).astype(np.float32)
    out = {}
    for k, v in d.items():
        if k == 'Zg_s':
            out['Zg_s_bytes'] = e4m3fn_bytes(x0 / s.astype(np.float64))
            out['Zg_s_scale'] = s
        else:
            out[k] = v
    return out


def reference(h_new, c_new, g_s, c_g_s, Wg_s, Zg_s_bytes, Zg_s_scale, bg_s):
    return core(h_new, c_new, g_s, c_g_s, Wg_s, e4m3fn_values(Zg_s_bytes) * Zg_s_scale.astype(np.float64), bg_s)

@@ -1,0 +1,220 @@
+from contextlib import ExitStack
+
+import concourse.mybir as mybir
+from concourse.masks import make_identity
+
+F32 = mybir.dt.float32
+BF16 = mybir.dt.bfloat16
+U32 = mybir.dt.uint32
+U8 = mybir.dt.uint8
+FP8 = mybir.dt.float8_e4m3fn
+FP8X4 = mybir.dt.float8_e4m3fn_x4
+ACT = mybir.ActivationFunctionType
+ALU = mybir.AluOpType
+
+P = 128
+B, T, NB, H, GH = 32, 4, 8, 512, 3
+FT = H // P
+UNITS = GH * T
+COLS = NB * B
+
+FLOPS = 2 * (B * NB + B) * H * H * GH * T
+
+
+def tile_st_hmr_pc_kernel(tc, h_new, c_new, g_s, c_g_s, Wg_s, Zg_s_bytes, Zg_s_scale, bg_s, out_0, out_1):
+    nc = tc.nc
+    with ExitStack() as ctx:
+        const = ctx.enter_context(tc.tile_pool(name="const", bufs=1))
+        raw = ctx.enter_context(tc.tile_pool(name="raw", bufs=6))
+        work = ctx.enter_context(tc.tile_pool(name="work", bufs=3))
+        codes = ctx.enter_context(tc.tile_pool(name="codes", bufs=4))
+        gates = ctx.enter_context(tc.tile_pool(name="gates", bufs=8))
+        mxps = ctx.enter_context(tc.psum_pool(name="mxps", bufs=4))
+        aux = ctx.enter_context(tc.psum_pool(name="aux", bufs=4))
+
+        warm = const.tile([P, 1], F32, name="warm")
+        nc.vector.memset(warm[:], 0.0)
+        nc.scalar.activation(out=warm[:], in_=warm[:], func=ACT.Sigmoid)
+        ident_f = const.tile([P, P], F32, name="ident_f")
+        make_identity(nc, ident_f[:])
+        ident_b = const.tile([P, P], BF16, name="ident_b")
+        make_identity(nc, ident_b[:])
+        bias_raw = const.tile([P, P], BF16, name="bias_raw")
+        nc.gpsimd.memset(bias_raw[:], 0.0)
+
+        zscale = const.tile([P, 4], F32, name="zscale")
+        h_sb = const.tile([P, NB, H], BF16, name="h_sb")
+        c_sb = const.tile([P, NB, H], BF16, name="c_sb")
+        gs_sb = const.tile([P, H], BF16, name="gs_sb")
+        cgs = const.tile([P, H], BF16, name="cgs")
+
+        zbytes = {}
+        wraw = {}
+        zwide = {}
+        wil = {}
+        zil = {}
+        wq = {}
+        zq = {}
+        mxp = {}
+        gate = {}
+
+        def load_z(u):
+            zbytes[u] = raw.tile([P, 4, H], U8, name="zbytes", tag="zbytes")
+            nc.sync.dma_start(out=zbytes[u][:], in_=Zg_s_bytes[u // T, u % T].rearrange("(p j) n -> p j n", j=4))
+
+        def load_w(u):
+            wraw[u] = raw.tile([P, 4, H], BF16, name="wraw", tag="wraw")
+            nc.sync.dma_start(out=wraw[u][:], in_=Wg_s[u // T, u % T].rearrange("(p j) n -> p j n", j=4))
+
+        def widen(u):
+            zwide[u] = work.tile([P, 4, H], BF16, name="zwide", tag="zwide")
+            for j in range(4):
+                nc.scalar.activation(out=zwide[u][:, j, :], in_=zbytes[u][:, j, :].bitcast(FP8), func=ACT.Copy,
+                                     scale=zscale[:, j:j + 1])
+
+        def il_z(u):
+            zil[u] = work.tile([P, H, 4], BF16, name="zil", tag="zil", align_bytes=64)
+            nc.vector.tensor_copy(out=zil[u][:], in_=zwide[u][:].rearrange("p j c -> p c j"))
+
+        def il_w(u):
+            wil[u] = work.tile([P, H, 4], BF16, name="wil", tag="wil", align_bytes=64)
+            nc.vector.tensor_copy(out=wil[u][:], in_=wraw[u][:].rearrange("p j c -> p c j"))
+
+        def quant(src, store, u, nm):
+            q = codes.tile([P, H], U32, name=nm + "q", tag=nm + "q", align_bytes=64)
+            s = codes.tile([P, H], U8, name=nm + "s", tag=nm + "s", align_bytes=64)
+            nc.vector.quantize_mx(out=q[:].bitcast(FP8X4), scales=s[:], in_=src[u][:].rearrange("p c j -> p (c j)"))
+            store[u] = (q, s)
+
+        def mm(u):
+            t = u % T
+            cols = slice(t * COLS, (t + 1) * COLS)
+            for ft in range(FT):
+                if ft % 2 == 0:
+                    mxp[(u, ft // 2)] = mxps.tile([P, 2, COLS], F32, name="mxp", tag="mxp")
+                acc = mxp[(u, ft // 2)][:, ft % 2, :]
+                fs = slice(ft * P, (ft + 1) * P)
+                nc.tensor.matmul_mx(out=acc, lhsT=wq[u][0][:, fs].bitcast(FP8X4), lhsT_scale=wq[u][1][:, fs],
+                                    rhs=hq[:, cols].bitcast(FP8X4), rhs_scale=hs[:, cols], start=True, stop=False)
+                nc.tensor.matmul_mx(out=acc, lhsT=zq[u][0][:, fs].bitcast(FP8X4), lhsT_scale=zq[u][1][:, fs],
+                                    rhs=gq[:, cols].bitcast(FP8X4), rhs_scale=gsc[:, cols], start=False, stop=True)
+
+        def sig(u):
+            g, t = u // T, u % T
+            for ft in range(FT):
+                if t == 0:
+                    gate[(g, ft)] = gates.tile([P, NB, T, B], F32, name="gate", tag="gate")
+                col = u * FT + ft
+                nc.scalar.activation(out=gate[(g, ft)][:, :, t, :],
+                                     in_=mxp[(u, ft // 2)][:, ft % 2, :].rearrange("p (n b) -> p n b", b=B),
+                                     func=ACT.Sigmoid, bias=bias_sb[:, col:col + 1], scale=1.0)
+
+        def reduce_gate(g):
+            acc = aux.tile([P, H], F32, name="acc", tag="aux")
+            for ft in range(FT):
+                for n in range(NB):
+                    nc.tensor.matmul(out=acc[:, ft * P:(ft + 1) * P],
+                                     lhsT=gate[(g, ft)][:, n].rearrange("p t b -> p (t b)"), rhs=ident_f[:],
+                                     is_transpose=True, start=(n == 0), stop=(n == NB - 1))
+            return acc
+
+        nc.sync.dma_start(out=zscale[:], in_=Zg_s_scale[0, 0].rearrange("(p j) c -> p (j c)", j=4))
+        load_z(0)
+        load_w(0)
+        load_z(1)
+        nc.sync.dma_start(out=h_sb[:], in_=h_new.rearrange("b t n h -> (b t) n h"))
+        nc.sync.dma_start(out=gs_sb[:], in_=g_s.rearrange("b t h -> (b t) h"))
+        nc.sync.dma_start(out=bias_raw[0:UNITS * FT, :], in_=bg_s.rearrange("g t o (c f) -> (g t o c) f", f=P))
+        load_w(1)
+        load_z(2)
+        load_w(2)
+        nc.sync.dma_start(out=c_sb[:], in_=c_new.rearrange("b t n h -> (b t) n h"))
+        for u in range(3, 6):
+            load_z(u)
+            load_w(u)
+
+        widen(0)
+        il_w(0)
+
+        hin = const.tile([P, T * COLS * 4], BF16, name="hin", align_bytes=64)
+        gin = const.tile([P, T * COLS * 4], BF16, name="gin", align_bytes=64)
+        hq = const.tile([P, T * COLS], U32, name="hq", align_bytes=64)
+        hs = const.tile([P, T * COLS], U8, name="hs", align_bytes=64)
+        gq = const.tile([P, T * COLS], U32, name="gq", align_bytes=64)
+        gsc = const.tile([P, T * COLS], U8, name="gsc", align_bytes=64)
+        hin_w = hin[:].bitcast(F32).rearrange("p (t n b u) -> p t n b u", t=T, n=NB, b=B, u=2)
+        gin_w = gin[:].bitcast(F32).rearrange("p (t n b u) -> p t n b u", t=T, n=NB, b=B, u=2)
+        hw = h_sb[:].bitcast(F32)
+        hT = None
+        for n in range(NB):
+            if n % 2 == 0:
+                hT = aux.tile([P, 2, 2, P], F32, name="hT", tag="aux")
+            for u in range(2):
+                nc.tensor.transpose(hT[:, n % 2, u, :], hw[:, n, u::2], ident_f[:])
+            nc.scalar.copy(out=hin_w[:, :, n, :, :], in_=hT[:, n % 2].rearrange("p u (b t) -> p t b u", t=T))
+        gw = gs_sb[:].bitcast(F32)
+        gT = aux.tile([P, 2, P], F32, name="gT", tag="aux")
+        for u in range(2):
+            nc.tensor.transpose(gT[:, u, :], gw[:, u::2], ident_f[:])
+        gT_v = gT[:].rearrange("p u (b t) -> p t b u", t=T)
+        for t in range(T):
+            nc.scalar.copy(out=gin_w[:, t], in_=gT_v[:, t].unsqueeze(1).to_broadcast([P, NB, B, 2]))
+        bT = aux.tile([P, P], BF16, name="bT", tag="aux")
+        nc.tensor.transpose(bT[:], bias_raw[:], ident_b[:])
+        bias_sb = const.tile([P, UNITS * FT], F32, name="bias_sb")
+        nc.vector.tensor_copy(out=bias_sb[:], in_=bT[:, 0:UNITS * FT])
+        nc.vector.quantize_mx(out=hq[:].bitcast(FP8X4), scales=hs[:], in_=hin[:])
+        nc.vector.quantize_mx(out=gq[:].bitcast(FP8X4), scales=gsc[:], in_=gin[:])
+
+        cT = {}
+        t1 = const.tile([P, H], F32, name="t1")
+        cnew = const.tile([P, H], F32, name="cnew")
+        s2 = const.tile([P, H], F32, name="s2")
+        gnew = const.tile([P, H], F32, name="gnew")
+        acc_fc = None
+
+        for i in range(0, UNITS + 1):
+            if i + 1 < UNITS:
+                widen(i + 1)
+            if i >= 1:
+                sig(i - 1)
+            if i < UNITS:
+                il_z(i)
+                quant(wil, wq, i, "w")
+            if i + 1 < UNITS:
+                il_w(i + 1)
+            if i < UNITS:
+                quant(zil, zq, i, "z")
+                mm(i)
+            if i == 1:
+                for ft in range(FT):
+                    cT[ft] = aux.tile([P, NB, P], BF16, name="cT", tag="aux")
+                    for n in range(NB):
+                        nc.tensor.transpose(cT[ft][:, n, :], c_sb[:, n, ft * P:(ft + 1) * P], ident_b[:])
+            if i == 4:
+                for ft in range(FT):
+                    f = gate[(0, ft)]
+                    nc.vector.tensor_tensor(out=f[:], in0=f[:], in1=cT[ft][:].rearrange("p n (b t) -> p n t b", t=T),
+                                            op=ALU.mult)
+                acc_fc = reduce_gate(0)
+            if i == 8:
+                acc_gg = reduce_gate(1)
+                nc.vector.scalar_tensor_tensor(out=t1[:], in0=acc_gg[:], scalar=0.125, in1=cgs[:], op0=ALU.mult,
+                                               op1=ALU.mult)
+                nc.vector.scalar_tensor_tensor(out=cnew[:], in0=acc_fc[:], scalar=0.125, in1=t1[:], op0=ALU.mult,
+                                               op1=ALU.add)
+                for t in range(T):
+                    nc.sync.dma_start(out=out_1[:, t, :], in_=cnew[t * B:(t + 1) * B, :])
+                nc.scalar.activation(out=s2[:], in_=cnew[:], func=ACT.Sigmoid, scale=2.0)
+                nc.vector.tensor_scalar(out=s2[:], in0=s2[:], scalar1=0.25, scalar2=-0.125, op0=ALU.mult, op1=ALU.add)
+            if i == UNITS:
+                acc_o = reduce_gate(2)
+                nc.vector.tensor_tensor(out=gnew[:], in0=acc_o[:], in1=s2[:], op=ALU.mult)
+                for t in range(T):
+                    nc.sync.dma_start(out=out_0[:, t, :], in_=gnew[t * B:(t + 1) * B, :])
+            if i + 6 < UNITS:
+                load_z(i + 6)
+                load_w(i + 6)
+            if i == 5:
+                for t in range(T):
+                    nc.sync.dma_start(out=cgs[t * B:(t + 1) * B, :], in_=c_g_s[:, t, :])

@@ -5,18 +5,24 @@ from concourse.masks import make_identity
 
 F32 = mybir.dt.float32
 BF16 = mybir.dt.bfloat16
+I32 = mybir.dt.int32
 U32 = mybir.dt.uint32
 U8 = mybir.dt.uint8
 FP8 = mybir.dt.float8_e4m3fn
 FP8X4 = mybir.dt.float8_e4m3fn_x4
 ACT = mybir.ActivationFunctionType
 ALU = mybir.AluOpType
+AX = mybir.AxisListType
 
 P = 128
 B, T, NB, H, GH = 32, 4, 8, 512, 3
 FT = H // P
 UNITS = GH * T
 COLS = NB * B
+LEAD = 2
+RAWBUFS = 6
+SHARE_W = [0, 0, 0, 0, 0, 0, 224, 224, 192, 192, 192, 192]
+FC_SLOT = [4, 5, 6, 7]
 
 FLOPS = 2 * (B * NB + B) * H * H * GH * T
 
@@ -25,12 +31,12 @@ def tile_st_hmr_pc_kernel(tc, h_new, c_new, g_s, c_g_s, Wg_s, Zg_s_bytes, Zg_s_s
     nc = tc.nc
     with ExitStack() as ctx:
         const = ctx.enter_context(tc.tile_pool(name="const", bufs=1))
-        raw = ctx.enter_context(tc.tile_pool(name="raw", bufs=6))
-        work = ctx.enter_context(tc.tile_pool(name="work", bufs=3))
+        raw = ctx.enter_context(tc.tile_pool(name="raw", bufs=RAWBUFS))
+        work = ctx.enter_context(tc.tile_pool(name="work", bufs=4))
         codes = ctx.enter_context(tc.tile_pool(name="codes", bufs=4))
-        gates = ctx.enter_context(tc.tile_pool(name="gates", bufs=8))
         mxps = ctx.enter_context(tc.psum_pool(name="mxps", bufs=4))
         aux = ctx.enter_context(tc.psum_pool(name="aux", bufs=4))
+        ctx.enter_context(tc.manual_schedule())
 
         warm = const.tile([P, 1], F32, name="warm")
         nc.vector.memset(warm[:], 0.0)
@@ -41,12 +47,35 @@ def tile_st_hmr_pc_kernel(tc, h_new, c_new, g_s, c_g_s, Wg_s, Zg_s_bytes, Zg_s_s
         make_identity(nc, ident_b[:])
         bias_raw = const.tile([P, P], BF16, name="bias_raw")
         nc.gpsimd.memset(bias_raw[:], 0.0)
+        r3 = const.tile([P, FT, P], F32, name="r3")
+        nc.gpsimd.memset(r3[:], 0.0)
+        gs0 = const.tile([P, T * B], U8, name="gs0", align_bytes=64)
+        nc.vector.memset(gs0[:].bitcast(I32), 0)
 
         zscale = const.tile([P, 4], F32, name="zscale")
         h_sb = const.tile([P, NB, H], BF16, name="h_sb")
         c_sb = const.tile([P, NB, H], BF16, name="c_sb")
         gs_sb = const.tile([P, H], BF16, name="gs_sb")
         cgs = const.tile([P, H], BF16, name="cgs")
+        bias_sb = const.tile([P, UNITS * FT], F32, name="bias_sb")
+        hin = const.tile([P, T * COLS * 4], BF16, name="hin", align_bytes=64)
+        gin0 = const.tile([P, T * B * 4], BF16, name="gin0", align_bytes=64)
+        hq = const.tile([P, T * COLS], U32, name="hq", align_bytes=64)
+        hs = const.tile([P, T * COLS], U8, name="hs", align_bytes=64)
+        gq0 = const.tile([P, T * B], U32, name="gq0", align_bytes=64)
+        gq = const.tile([P, T * COLS], U32, name="gq", align_bytes=64)
+        gsc = const.tile([P, T * COLS], U8, name="gsc", align_bytes=64)
+        t1 = const.tile([P, H], F32, name="t1")
+        cnew = const.tile([P, H], F32, name="cnew")
+        s2 = const.tile([P, H], F32, name="s2")
+        gnew = const.tile([P, H], F32, name="gnew")
+        gate_a = {}
+        gate_b = {}
+        last = {}
+        for ft in range(FT):
+            gate_a[ft] = const.tile([P, NB, T, B], F32, name="gate_a%d" % ft)
+            gate_b[ft] = const.tile([P, NB, T, B], F32, name="gate_b%d" % ft)
+            last[ft] = const.tile([P, NB, B], F32, name="last%d" % ft)
 
         zbytes = {}
         wraw = {}
@@ -56,7 +85,8 @@ def tile_st_hmr_pc_kernel(tc, h_new, c_new, g_s, c_g_s, Wg_s, Zg_s_bytes, Zg_s_s
         wq = {}
         zq = {}
         mxp = {}
-        gate = {}
+        cT = {}
+        acc = {}
 
         def load_z(u):
             zbytes[u] = raw.tile([P, 4, H], U8, name="zbytes", tag="zbytes")
@@ -72,13 +102,23 @@ def tile_st_hmr_pc_kernel(tc, h_new, c_new, g_s, c_g_s, Wg_s, Zg_s_bytes, Zg_s_s
                 nc.scalar.activation(out=zwide[u][:, j, :], in_=zbytes[u][:, j, :].bitcast(FP8), func=ACT.Copy,
                                      scale=zscale[:, j:j + 1])
 
+        def wil_tile(u):
+            if u not in wil:
+                wil[u] = work.tile([P, H, 4], BF16, name="wil", tag="wil", align_bytes=64)
+            return wil[u]
+
+        def il_w_scalar(u):
+            c0 = H - SHARE_W[u]
+            if c0 < H:
+                nc.scalar.copy(out=wil_tile(u)[:, c0:H, :], in_=wraw[u][:, :, c0:H].rearrange("p j c -> p c j"))
+
+        def il_w(u):
+            c0 = H - SHARE_W[u]
+            nc.vector.tensor_copy(out=wil_tile(u)[:, 0:c0, :], in_=wraw[u][:, :, 0:c0].rearrange("p j c -> p c j"))
+
         def il_z(u):
             zil[u] = work.tile([P, H, 4], BF16, name="zil", tag="zil", align_bytes=64)
             nc.vector.tensor_copy(out=zil[u][:], in_=zwide[u][:].rearrange("p j c -> p c j"))
-
-        def il_w(u):
-            wil[u] = work.tile([P, H, 4], BF16, name="wil", tag="wil", align_bytes=64)
-            nc.vector.tensor_copy(out=wil[u][:], in_=wraw[u][:].rearrange("p j c -> p c j"))
 
         def quant(src, store, u, nm):
             q = codes.tile([P, H], U32, name=nm + "q", tag=nm + "q", align_bytes=64)
@@ -92,92 +132,86 @@ def tile_st_hmr_pc_kernel(tc, h_new, c_new, g_s, c_g_s, Wg_s, Zg_s_bytes, Zg_s_s
             for ft in range(FT):
                 if ft % 2 == 0:
                     mxp[(u, ft // 2)] = mxps.tile([P, 2, COLS], F32, name="mxp", tag="mxp")
-                acc = mxp[(u, ft // 2)][:, ft % 2, :]
+                ps = mxp[(u, ft // 2)][:, ft % 2, :]
                 fs = slice(ft * P, (ft + 1) * P)
-                nc.tensor.matmul_mx(out=acc, lhsT=wq[u][0][:, fs].bitcast(FP8X4), lhsT_scale=wq[u][1][:, fs],
+                nc.tensor.matmul_mx(out=ps, lhsT=wq[u][0][:, fs].bitcast(FP8X4), lhsT_scale=wq[u][1][:, fs],
                                     rhs=hq[:, cols].bitcast(FP8X4), rhs_scale=hs[:, cols], start=True, stop=False)
-                nc.tensor.matmul_mx(out=acc, lhsT=zq[u][0][:, fs].bitcast(FP8X4), lhsT_scale=zq[u][1][:, fs],
+                nc.tensor.matmul_mx(out=ps, lhsT=zq[u][0][:, fs].bitcast(FP8X4), lhsT_scale=zq[u][1][:, fs],
                                     rhs=gq[:, cols].bitcast(FP8X4), rhs_scale=gsc[:, cols], start=False, stop=True)
 
         def sig(u):
             g, t = u // T, u % T
             for ft in range(FT):
-                if t == 0:
-                    gate[(g, ft)] = gates.tile([P, NB, T, B], F32, name="gate", tag="gate")
+                if u == UNITS - 1:
+                    dst = last[ft][:]
+                elif g == 1:
+                    dst = gate_b[ft][:, :, t, :]
+                else:
+                    dst = gate_a[ft][:, :, t, :]
                 col = u * FT + ft
-                nc.scalar.activation(out=gate[(g, ft)][:, :, t, :],
-                                     in_=mxp[(u, ft // 2)][:, ft % 2, :].rearrange("p (n b) -> p n b", b=B),
+                nc.scalar.activation(out=dst, in_=mxp[(u, ft // 2)][:, ft % 2, :].rearrange("p (n b) -> p n b", b=B),
                                      func=ACT.Sigmoid, bias=bias_sb[:, col:col + 1], scale=1.0)
 
-        def reduce_gate(g):
-            acc = aux.tile([P, H], F32, name="acc", tag="aux")
-            for ft in range(FT):
-                for n in range(NB):
-                    nc.tensor.matmul(out=acc[:, ft * P:(ft + 1) * P],
-                                     lhsT=gate[(g, ft)][:, n].rearrange("p t b -> p (t b)"), rhs=ident_f[:],
-                                     is_transpose=True, start=(n == 0), stop=(n == NB - 1))
-            return acc
+        def reduce_gate(g, ft):
+            if ft == 0:
+                acc[g] = aux.tile([P, H], F32, name="acc", tag="aux")
+            src = gate_b[ft] if g == 1 else gate_a[ft]
+            for n in range(NB):
+                nc.tensor.matmul(out=acc[g][:, ft * P:(ft + 1) * P], lhsT=src[:, n].rearrange("p t b -> p (t b)"),
+                                 rhs=ident_f[:], is_transpose=True, start=(n == 0), stop=(n == NB - 1))
 
         nc.sync.dma_start(out=zscale[:], in_=Zg_s_scale[0, 0].rearrange("(p j) c -> p (j c)", j=4))
         load_z(0)
         load_w(0)
         load_z(1)
+        load_w(1)
         nc.sync.dma_start(out=h_sb[:], in_=h_new.rearrange("b t n h -> (b t) n h"))
         nc.sync.dma_start(out=gs_sb[:], in_=g_s.rearrange("b t h -> (b t) h"))
         nc.sync.dma_start(out=bias_raw[0:UNITS * FT, :], in_=bg_s.rearrange("g t o (c f) -> (g t o c) f", f=P))
-        load_w(1)
         load_z(2)
         load_w(2)
+        load_z(3)
+        load_w(3)
         nc.sync.dma_start(out=c_sb[:], in_=c_new.rearrange("b t n h -> (b t) n h"))
-        for u in range(3, 6):
+        for u in range(4, RAWBUFS):
             load_z(u)
             load_w(u)
 
-        widen(0)
+        for u in range(LEAD):
+            widen(u)
+        il_w_scalar(0)
         il_w(0)
 
-        hin = const.tile([P, T * COLS * 4], BF16, name="hin", align_bytes=64)
-        gin = const.tile([P, T * COLS * 4], BF16, name="gin", align_bytes=64)
-        hq = const.tile([P, T * COLS], U32, name="hq", align_bytes=64)
-        hs = const.tile([P, T * COLS], U8, name="hs", align_bytes=64)
-        gq = const.tile([P, T * COLS], U32, name="gq", align_bytes=64)
-        gsc = const.tile([P, T * COLS], U8, name="gsc", align_bytes=64)
         hin_w = hin[:].bitcast(F32).rearrange("p (t n b u) -> p t n b u", t=T, n=NB, b=B, u=2)
-        gin_w = gin[:].bitcast(F32).rearrange("p (t n b u) -> p t n b u", t=T, n=NB, b=B, u=2)
-        hw = h_sb[:].bitcast(F32)
-        hT = None
-        for n in range(NB):
-            if n % 2 == 0:
-                hT = aux.tile([P, 2, 2, P], F32, name="hT", tag="aux")
-            for u in range(2):
-                nc.tensor.transpose(hT[:, n % 2, u, :], hw[:, n, u::2], ident_f[:])
-            nc.scalar.copy(out=hin_w[:, :, n, :, :], in_=hT[:, n % 2].rearrange("p u (b t) -> p t b u", t=T))
-        gw = gs_sb[:].bitcast(F32)
-        gT = aux.tile([P, 2, P], F32, name="gT", tag="aux")
-        for u in range(2):
-            nc.tensor.transpose(gT[:, u, :], gw[:, u::2], ident_f[:])
-        gT_v = gT[:].rearrange("p u (b t) -> p t b u", t=T)
-        for t in range(T):
-            nc.scalar.copy(out=gin_w[:, t], in_=gT_v[:, t].unsqueeze(1).to_broadcast([P, NB, B, 2]))
-        bT = aux.tile([P, P], BF16, name="bT", tag="aux")
-        nc.tensor.transpose(bT[:], bias_raw[:], ident_b[:])
-        bias_sb = const.tile([P, UNITS * FT], F32, name="bias_sb")
-        nc.vector.tensor_copy(out=bias_sb[:], in_=bT[:, 0:UNITS * FT])
-        nc.vector.quantize_mx(out=hq[:].bitcast(FP8X4), scales=hs[:], in_=hin[:])
-        nc.vector.quantize_mx(out=gq[:].bitcast(FP8X4), scales=gsc[:], in_=gin[:])
-
-        cT = {}
-        t1 = const.tile([P, H], F32, name="t1")
-        cnew = const.tile([P, H], F32, name="cnew")
-        s2 = const.tile([P, H], F32, name="s2")
-        gnew = const.tile([P, H], F32, name="gnew")
-        acc_fc = None
-
-        for i in range(0, UNITS + 1):
+        next_sig = 0
+        issued_mm = 0
+        for i in range(UNITS + 1):
+            if i == 0:
+                hw = h_sb[:].bitcast(F32)
+                hT = None
+                for n in range(NB):
+                    if n % 2 == 0:
+                        hT = aux.tile([P, 2, 2, P], F32, name="hT", tag="aux")
+                    for u in range(2):
+                        nc.tensor.transpose(hT[:, n % 2, u, :], hw[:, n, u::2], ident_f[:])
+                    nc.scalar.copy(out=hin_w[:, :, n, :, :], in_=hT[:, n % 2].rearrange("p u (b t) -> p t b u", t=T))
+                gw = gs_sb[:].bitcast(F32)
+                gT = aux.tile([P, 2, P], F32, name="gT", tag="aux")
+                for u in range(2):
+                    nc.tensor.transpose(gT[:, u, :], gw[:, u::2], ident_f[:])
+                bT = aux.tile([P, P], BF16, name="bT", tag="aux")
+                nc.tensor.transpose(bT[:], bias_raw[:], ident_b[:])
+                nc.scalar.copy(out=gin0[:].bitcast(F32).rearrange("p (t b u) -> p t b u", t=T, b=B, u=2),
+                               in_=gT[:].rearrange("p u (b t) -> p t b u", t=T))
+            if i + LEAD < UNITS:
+                widen(i + LEAD)
             if i + 1 < UNITS:
-                widen(i + 1)
-            if i >= 1:
-                sig(i - 1)
+                il_w_scalar(i + 1)
+            for k in range(min(2, issued_mm - next_sig)):
+                sig(next_sig)
+                next_sig += 1
+            if i == UNITS - 1:
+                nc.scalar.activation(out=s2[:], in_=cnew[:], func=ACT.Sigmoid, scale=2.0)
             if i < UNITS:
                 il_z(i)
                 quant(wil, wq, i, "w")
@@ -185,36 +219,65 @@ def tile_st_hmr_pc_kernel(tc, h_new, c_new, g_s, c_g_s, Wg_s, Zg_s_bytes, Zg_s_s
                 il_w(i + 1)
             if i < UNITS:
                 quant(zil, zq, i, "z")
-                mm(i)
             if i == 1:
+                nc.vector.tensor_copy(out=bias_sb[:], in_=bT[:, 0:UNITS * FT])
+                nc.vector.quantize_mx(out=hq[:].bitcast(FP8X4), scales=hs[:], in_=hin[:])
+                nc.vector.quantize_mx(out=gq0[:].bitcast(FP8X4), scales=gs0[:], in_=gin0[:])
+                nc.vector.tensor_copy(
+                    out=gq[:].bitcast(I32).rearrange("p (t n b) -> p t n b", t=T, n=NB, b=B),
+                    in_=gq0[:].bitcast(I32).rearrange("p (t b) -> p t b", t=T).unsqueeze(2).to_broadcast([P, T, NB, B]))
+                nc.vector.tensor_copy(
+                    out=gsc[:].bitcast(I32).rearrange("p (t n w) -> p t n w", t=T, n=NB, w=B // 4),
+                    in_=gs0[:].bitcast(I32).rearrange("p (t w) -> p t w", t=T).unsqueeze(2).to_broadcast(
+                        [P, T, NB, B // 4]))
+                mm(0)
+                issued_mm += 1
+            if 1 <= i < UNITS:
+                mm(i)
+                issued_mm += 1
+            if i == 2:
                 for ft in range(FT):
                     cT[ft] = aux.tile([P, NB, P], BF16, name="cT", tag="aux")
                     for n in range(NB):
                         nc.tensor.transpose(cT[ft][:, n, :], c_sb[:, n, ft * P:(ft + 1) * P], ident_b[:])
-            if i == 4:
-                for ft in range(FT):
-                    f = gate[(0, ft)]
+            for ft in range(FT):
+                if FC_SLOT[ft] == i:
+                    f = gate_a[ft]
                     nc.vector.tensor_tensor(out=f[:], in0=f[:], in1=cT[ft][:].rearrange("p n (b t) -> p n t b", t=T),
                                             op=ALU.mult)
-                acc_fc = reduce_gate(0)
+                    reduce_gate(0, ft)
             if i == 8:
-                acc_gg = reduce_gate(1)
-                nc.vector.scalar_tensor_tensor(out=t1[:], in0=acc_gg[:], scalar=0.125, in1=cgs[:], op0=ALU.mult,
+                reduce_gate(1, 0)
+                reduce_gate(1, 1)
+            if i == 9:
+                reduce_gate(1, 2)
+                reduce_gate(1, 3)
+            if i == 10:
+                nc.vector.scalar_tensor_tensor(out=t1[:], in0=acc[1][:], scalar=0.125, in1=cgs[:], op0=ALU.mult,
                                                op1=ALU.mult)
-                nc.vector.scalar_tensor_tensor(out=cnew[:], in0=acc_fc[:], scalar=0.125, in1=t1[:], op0=ALU.mult,
+                nc.vector.scalar_tensor_tensor(out=cnew[:], in0=acc[0][:], scalar=0.125, in1=t1[:], op0=ALU.mult,
                                                op1=ALU.add)
                 for t in range(T):
                     nc.sync.dma_start(out=out_1[:, t, :], in_=cnew[t * B:(t + 1) * B, :])
-                nc.scalar.activation(out=s2[:], in_=cnew[:], func=ACT.Sigmoid, scale=2.0)
-                nc.vector.tensor_scalar(out=s2[:], in0=s2[:], scalar1=0.25, scalar2=-0.125, op0=ALU.mult, op1=ALU.add)
-            if i == UNITS:
-                acc_o = reduce_gate(2)
-                nc.vector.tensor_tensor(out=gnew[:], in0=acc_o[:], in1=s2[:], op=ALU.mult)
-                for t in range(T):
-                    nc.sync.dma_start(out=out_0[:, t, :], in_=gnew[t * B:(t + 1) * B, :])
-            if i + 6 < UNITS:
-                load_z(i + 6)
-                load_w(i + 6)
-            if i == 5:
+                sig(next_sig)
+                next_sig += 1
+                for ft in range(FT):
+                    reduce_gate(2, ft)
+            if i + RAWBUFS < UNITS:
+                load_z(i + RAWBUFS)
+                load_w(i + RAWBUFS)
+            if i == 4:
                 for t in range(T):
                     nc.sync.dma_start(out=cgs[t * B:(t + 1) * B, :], in_=c_g_s[:, t, :])
+
+        R = (T - 1) * B
+        nc.vector.tensor_scalar(out=s2[:], in0=s2[:], scalar1=0.25, scalar2=-0.125, op0=ALU.mult, op1=ALU.add)
+        nc.vector.tensor_tensor(out=gnew[0:R, :], in0=acc[2][0:R, :], in1=s2[0:R, :], op=ALU.mult)
+        for t in range(T - 1):
+            nc.sync.dma_start(out=out_0[:, t, :], in_=gnew[t * B:(t + 1) * B, :])
+        acc3 = aux.tile([P, H], F32, name="acc3", tag="aux")
+        for ft in range(FT):
+            nc.vector.tensor_reduce(out=r3[:, ft, R:P], in_=last[ft][:].rearrange("p n b -> p b n"), axis=AX.X, op=ALU.add)
+            nc.tensor.transpose(acc3[:, ft * P:(ft + 1) * P], r3[:, ft, :], ident_f[:])
+        nc.vector.tensor_tensor(out=gnew[R:P, :], in0=acc3[R:P, :], in1=s2[R:P, :], op=ALU.mult)
+        nc.sync.dma_start(out=out_0[:, T - 1, :], in_=gnew[R:P, :])

@@ -23,6 +23,7 @@ LEAD = 2
 RAWBUFS = 6
 SHARE_W = [0, 0, 0, 0, 0, 0, 224, 224, 192, 192, 192, 192]
 FC_SLOT = [4, 5, 6, 7]
+FILLERS = [0, 5, 9, 6, 3, 3, 3, 6, 4, 4, 0, 0, 0]
 
 FLOPS = 2 * (B * NB + B) * H * H * GH * T
 
@@ -35,7 +36,7 @@ def tile_st_hmr_pc_kernel(tc, h_new, c_new, g_s, c_g_s, Wg_s, Zg_s_bytes, Zg_s_s
         work = ctx.enter_context(tc.tile_pool(name="work", bufs=4))
         codes = ctx.enter_context(tc.tile_pool(name="codes", bufs=4))
         mxps = ctx.enter_context(tc.psum_pool(name="mxps", bufs=4))
-        aux = ctx.enter_context(tc.psum_pool(name="aux", bufs=4))
+        aux = ctx.enter_context(tc.psum_pool(name="aux", bufs=1))
         ctx.enter_context(tc.manual_schedule())
 
         warm = const.tile([P, 1], F32, name="warm")
@@ -154,7 +155,7 @@ def tile_st_hmr_pc_kernel(tc, h_new, c_new, g_s, c_g_s, Wg_s, Zg_s_bytes, Zg_s_s
 
         def reduce_gate(g, ft):
             if ft == 0:
-                acc[g] = aux.tile([P, H], F32, name="acc", tag="aux")
+                acc[g] = aux.tile([P, H], F32, name="acc", tag="acc", bufs=2)
             src = gate_b[ft] if g == 1 else gate_a[ft]
             for n in range(NB):
                 nc.tensor.matmul(out=acc[g][:, ft * P:(ft + 1) * P], lhsT=src[:, n].rearrange("p t b -> p (t b)"),
@@ -182,6 +183,7 @@ def tile_st_hmr_pc_kernel(tc, h_new, c_new, g_s, c_g_s, Wg_s, Zg_s_bytes, Zg_s_s
         il_w_scalar(0)
         il_w(0)
 
+        scratch = aux.tile([P, H], F32, name="scratch", tag="fill", bufs=1)
         hin_w = hin[:].bitcast(F32).rearrange("p (t n b u) -> p t n b u", t=T, n=NB, b=B, u=2)
         next_sig = 0
         issued_mm = 0
@@ -191,15 +193,18 @@ def tile_st_hmr_pc_kernel(tc, h_new, c_new, g_s, c_g_s, Wg_s, Zg_s_bytes, Zg_s_s
                 hT = None
                 for n in range(NB):
                     if n % 2 == 0:
-                        hT = aux.tile([P, 2, 2, P], F32, name="hT", tag="aux")
+                        if n in (0, 6):
+                            hT = aux.tile([P, 2, 2, P], F32, name="hT", tag="tp", bufs=1)
+                        else:
+                            hT = aux.tile([P, 2, 2, P], F32, name="hT", tag="acc", bufs=2)
                     for u in range(2):
                         nc.tensor.transpose(hT[:, n % 2, u, :], hw[:, n, u::2], ident_f[:])
                     nc.scalar.copy(out=hin_w[:, :, n, :, :], in_=hT[:, n % 2].rearrange("p u (b t) -> p t b u", t=T))
                 gw = gs_sb[:].bitcast(F32)
-                gT = aux.tile([P, 2, P], F32, name="gT", tag="aux")
+                gT = aux.tile([P, 2, P], F32, name="gT", tag="acc", bufs=2)
                 for u in range(2):
                     nc.tensor.transpose(gT[:, u, :], gw[:, u::2], ident_f[:])
-                bT = aux.tile([P, P], BF16, name="bT", tag="aux")
+                bT = aux.tile([P, P], BF16, name="bT", tag="acc", bufs=2)
                 nc.tensor.transpose(bT[:], bias_raw[:], ident_b[:])
                 nc.scalar.copy(out=gin0[:].bitcast(F32).rearrange("p (t b u) -> p t b u", t=T, b=B, u=2),
                                in_=gT[:].rearrange("p u (b t) -> p t b u", t=T))
@@ -235,17 +240,17 @@ def tile_st_hmr_pc_kernel(tc, h_new, c_new, g_s, c_g_s, Wg_s, Zg_s_bytes, Zg_s_s
             if 1 <= i < UNITS:
                 mm(i)
                 issued_mm += 1
-            if i == 2:
-                for ft in range(FT):
-                    cT[ft] = aux.tile([P, NB, P], BF16, name="cT", tag="aux")
-                    for n in range(NB):
-                        nc.tensor.transpose(cT[ft][:, n, :], c_sb[:, n, ft * P:(ft + 1) * P], ident_b[:])
             for ft in range(FT):
                 if FC_SLOT[ft] == i:
                     f = gate_a[ft]
                     nc.vector.tensor_tensor(out=f[:], in0=f[:], in1=cT[ft][:].rearrange("p n (b t) -> p n t b", t=T),
                                             op=ALU.mult)
                     reduce_gate(0, ft)
+            for ft in range(FT):
+                if FC_SLOT[ft] == i + 1:
+                    cT[ft] = aux.tile([P, NB, P], BF16, name="cT", tag="tp", bufs=1)
+                    for n in range(NB):
+                        nc.tensor.transpose(cT[ft][:, n, :], c_sb[:, n, ft * P:(ft + 1) * P], ident_b[:])
             if i == 8:
                 reduce_gate(1, 0)
                 reduce_gate(1, 1)
@@ -263,6 +268,9 @@ def tile_st_hmr_pc_kernel(tc, h_new, c_new, g_s, c_g_s, Wg_s, Zg_s_bytes, Zg_s_s
                 next_sig += 1
                 for ft in range(FT):
                     reduce_gate(2, ft)
+            for k in range(FILLERS[i]):
+                nc.tensor.matmul_mx(out=scratch[:], lhsT=wq[i][0][:, 0:P].bitcast(FP8X4), lhsT_scale=wq[i][1][:, 0:P],
+                                    rhs=hq[:, 0:H].bitcast(FP8X4), rhs_scale=hs[:, 0:H], start=True, stop=True)
             if i + RAWBUFS < UNITS:
                 load_z(i + RAWBUFS)
                 load_w(i + RAWBUFS)
@@ -275,7 +283,7 @@ def tile_st_hmr_pc_kernel(tc, h_new, c_new, g_s, c_g_s, Wg_s, Zg_s_bytes, Zg_s_s
         nc.vector.tensor_tensor(out=gnew[0:R, :], in0=acc[2][0:R, :], in1=s2[0:R, :], op=ALU.mult)
         for t in range(T - 1):
             nc.sync.dma_start(out=out_0[:, t, :], in_=gnew[t * B:(t + 1) * B, :])
-        acc3 = aux.tile([P, H], F32, name="acc3", tag="aux")
+        acc3 = aux.tile([P, H], F32, name="acc3", tag="acc", bufs=2)
         for ft in range(FT):
             nc.vector.tensor_reduce(out=r3[:, ft, R:P], in_=last[ft][:].rearrange("p n b -> p b n"), axis=AX.X, op=ALU.add)
             nc.tensor.transpose(acc3[:, ft * P:(ft + 1) * P], r3[:, ft, :], ident_f[:])

@@ -23,7 +23,6 @@ LEAD = 2
 RAWBUFS = 6
 SHARE_W = [0, 0, 0, 0, 0, 0, 224, 224, 192, 192, 192, 192]
 FC_SLOT = [4, 5, 6, 7]
-FILLERS = [0, 5, 9, 6, 3, 3, 3, 6, 4, 4, 0, 0, 0]
 
 FLOPS = 2 * (B * NB + B) * H * H * GH * T
 
@@ -36,7 +35,7 @@ def tile_st_hmr_pc_kernel(tc, h_new, c_new, g_s, c_g_s, Wg_s, Zg_s_bytes, Zg_s_s
         work = ctx.enter_context(tc.tile_pool(name="work", bufs=4))
         codes = ctx.enter_context(tc.tile_pool(name="codes", bufs=4))
         mxps = ctx.enter_context(tc.psum_pool(name="mxps", bufs=4))
-        aux = ctx.enter_context(tc.psum_pool(name="aux", bufs=1))
+        aux = ctx.enter_context(tc.psum_pool(name="aux", bufs=4))
         ctx.enter_context(tc.manual_schedule())
 
         warm = const.tile([P, 1], F32, name="warm")
@@ -111,15 +110,18 @@ def tile_st_hmr_pc_kernel(tc, h_new, c_new, g_s, c_g_s, Wg_s, Zg_s_bytes, Zg_s_s
         def il_w_scalar(u):
             c0 = H - SHARE_W[u]
             if c0 < H:
-                nc.scalar.copy(out=wil_tile(u)[:, c0:H, :], in_=wraw[u][:, :, c0:H].rearrange("p j c -> p c j"))
+                nc.scalar.copy(out=wil_tile(u)[:, c0:H, :].rearrange("p (g i) j -> p g j i", i=4),
+                               in_=wraw[u][:, :, c0:H].rearrange("p j (g i) -> p g j i", i=4))
 
         def il_w(u):
             c0 = H - SHARE_W[u]
-            nc.vector.tensor_copy(out=wil_tile(u)[:, 0:c0, :], in_=wraw[u][:, :, 0:c0].rearrange("p j c -> p c j"))
+            nc.vector.tensor_copy(out=wil_tile(u)[:, 0:c0, :].rearrange("p (g i) j -> p g j i", i=4),
+                                  in_=wraw[u][:, :, 0:c0].rearrange("p j (g i) -> p g j i", i=4))
 
         def il_z(u):
             zil[u] = work.tile([P, H, 4], BF16, name="zil", tag="zil", align_bytes=64)
-            nc.vector.tensor_copy(out=zil[u][:], in_=zwide[u][:].rearrange("p j c -> p c j"))
+            nc.vector.tensor_copy(out=zil[u][:].rearrange("p (g i) j -> p g j i", i=4),
+                                  in_=zwide[u][:].rearrange("p j (g i) -> p g j i", i=4))
 
         def quant(src, store, u, nm):
             q = codes.tile([P, H], U32, name=nm + "q", tag=nm + "q", align_bytes=64)
@@ -155,7 +157,7 @@ def tile_st_hmr_pc_kernel(tc, h_new, c_new, g_s, c_g_s, Wg_s, Zg_s_bytes, Zg_s_s
 
         def reduce_gate(g, ft):
             if ft == 0:
-                acc[g] = aux.tile([P, H], F32, name="acc", tag="acc", bufs=2)
+                acc[g] = aux.tile([P, H], F32, name="acc", tag="aux")
             src = gate_b[ft] if g == 1 else gate_a[ft]
             for n in range(NB):
                 nc.tensor.matmul(out=acc[g][:, ft * P:(ft + 1) * P], lhsT=src[:, n].rearrange("p t b -> p (t b)"),
@@ -183,7 +185,6 @@ def tile_st_hmr_pc_kernel(tc, h_new, c_new, g_s, c_g_s, Wg_s, Zg_s_bytes, Zg_s_s
         il_w_scalar(0)
         il_w(0)
 
-        scratch = aux.tile([P, H], F32, name="scratch", tag="fill", bufs=1)
         hin_w = hin[:].bitcast(F32).rearrange("p (t n b u) -> p t n b u", t=T, n=NB, b=B, u=2)
         next_sig = 0
         issued_mm = 0
@@ -193,18 +194,15 @@ def tile_st_hmr_pc_kernel(tc, h_new, c_new, g_s, c_g_s, Wg_s, Zg_s_bytes, Zg_s_s
                 hT = None
                 for n in range(NB):
                     if n % 2 == 0:
-                        if n in (0, 6):
-                            hT = aux.tile([P, 2, 2, P], F32, name="hT", tag="tp", bufs=1)
-                        else:
-                            hT = aux.tile([P, 2, 2, P], F32, name="hT", tag="acc", bufs=2)
+                        hT = aux.tile([P, 2, 2, P], F32, name="hT", tag="aux")
                     for u in range(2):
                         nc.tensor.transpose(hT[:, n % 2, u, :], hw[:, n, u::2], ident_f[:])
                     nc.scalar.copy(out=hin_w[:, :, n, :, :], in_=hT[:, n % 2].rearrange("p u (b t) -> p t b u", t=T))
                 gw = gs_sb[:].bitcast(F32)
-                gT = aux.tile([P, 2, P], F32, name="gT", tag="acc", bufs=2)
+                gT = aux.tile([P, 2, P], F32, name="gT", tag="aux")
                 for u in range(2):
                     nc.tensor.transpose(gT[:, u, :], gw[:, u::2], ident_f[:])
-                bT = aux.tile([P, P], BF16, name="bT", tag="acc", bufs=2)
+                bT = aux.tile([P, P], BF16, name="bT", tag="aux")
                 nc.tensor.transpose(bT[:], bias_raw[:], ident_b[:])
                 nc.scalar.copy(out=gin0[:].bitcast(F32).rearrange("p (t b u) -> p t b u", t=T, b=B, u=2),
                                in_=gT[:].rearrange("p u (b t) -> p t b u", t=T))
@@ -240,17 +238,17 @@ def tile_st_hmr_pc_kernel(tc, h_new, c_new, g_s, c_g_s, Wg_s, Zg_s_bytes, Zg_s_s
             if 1 <= i < UNITS:
                 mm(i)
                 issued_mm += 1
+            if i == 2:
+                for ft in range(FT):
+                    cT[ft] = aux.tile([P, NB, P], BF16, name="cT", tag="aux")
+                    for n in range(NB):
+                        nc.tensor.transpose(cT[ft][:, n, :], c_sb[:, n, ft * P:(ft + 1) * P], ident_b[:])
             for ft in range(FT):
                 if FC_SLOT[ft] == i:
                     f = gate_a[ft]
                     nc.vector.tensor_tensor(out=f[:], in0=f[:], in1=cT[ft][:].rearrange("p n (b t) -> p n t b", t=T),
                                             op=ALU.mult)
                     reduce_gate(0, ft)
-            for ft in range(FT):
-                if FC_SLOT[ft] == i + 1:
-                    cT[ft] = aux.tile([P, NB, P], BF16, name="cT", tag="tp", bufs=1)
-                    for n in range(NB):
-                        nc.tensor.transpose(cT[ft][:, n, :], c_sb[:, n, ft * P:(ft + 1) * P], ident_b[:])
             if i == 8:
                 reduce_gate(1, 0)
                 reduce_gate(1, 1)
@@ -268,9 +266,6 @@ def tile_st_hmr_pc_kernel(tc, h_new, c_new, g_s, c_g_s, Wg_s, Zg_s_bytes, Zg_s_s
                 next_sig += 1
                 for ft in range(FT):
                     reduce_gate(2, ft)
-            for k in range(FILLERS[i]):
-                nc.tensor.matmul_mx(out=scratch[:], lhsT=wq[i][0][:, 0:P].bitcast(FP8X4), lhsT_scale=wq[i][1][:, 0:P],
-                                    rhs=hq[:, 0:H].bitcast(FP8X4), rhs_scale=hs[:, 0:H], start=True, stop=True)
             if i + RAWBUFS < UNITS:
                 load_z(i + RAWBUFS)
                 load_w(i + RAWBUFS)
@@ -283,7 +278,7 @@ def tile_st_hmr_pc_kernel(tc, h_new, c_new, g_s, c_g_s, Wg_s, Zg_s_bytes, Zg_s_s
         nc.vector.tensor_tensor(out=gnew[0:R, :], in0=acc[2][0:R, :], in1=s2[0:R, :], op=ALU.mult)
         for t in range(T - 1):
             nc.sync.dma_start(out=out_0[:, t, :], in_=gnew[t * B:(t + 1) * B, :])
-        acc3 = aux.tile([P, H], F32, name="acc3", tag="acc", bufs=2)
+        acc3 = aux.tile([P, H], F32, name="acc3", tag="aux")
         for ft in range(FT):
             nc.vector.tensor_reduce(out=r3[:, ft, R:P], in_=last[ft][:].rearrange("p n b -> p b n"), axis=AX.X, op=ALU.add)
             nc.tensor.transpose(acc3[:, ft * P:(ft + 1) * P], r3[:, ft, :], ident_f[:])

@@ -193,11 +193,10 @@ def tile_st_hmr_pc_kernel(tc, h_new, c_new, g_s, c_g_s, Wg_s, Zg_s_bytes, Zg_s_s
                 hw = h_sb[:].bitcast(F32)
                 hT = None
                 for n in range(NB):
-                    if n % 2 == 0:
-                        hT = aux.tile([P, 2, 2, P], F32, name="hT", tag="aux")
+                    hT = aux.tile([P, 2, P], F32, name="hT", tag="aux")
                     for u in range(2):
-                        nc.tensor.transpose(hT[:, n % 2, u, :], hw[:, n, u::2], ident_f[:])
-                    nc.scalar.copy(out=hin_w[:, :, n, :, :], in_=hT[:, n % 2].rearrange("p u (b t) -> p t b u", t=T))
+                        nc.tensor.transpose(hT[:, u, :], hw[:, n, u::2], ident_f[:])
+                    nc.scalar.copy(out=hin_w[:, :, n, :, :], in_=hT[:].rearrange("p u (b t) -> p t b u", t=T))
                 gw = gs_sb[:].bitcast(F32)
                 gT = aux.tile([P, 2, P], F32, name="gT", tag="aux")
                 for u in range(2):

@@ -19,11 +19,44 @@ B, T, NB, H, GH = 32, 4, 8, 512, 3
 FT = H // P
 UNITS = GH * T
 COLS = NB * B
-LEAD = 2
-RAWBUFS = 6
-SHARE_W = [0, 0, 0, 0, 0, 0, 224, 224, 192, 192, 192, 192]
-FC_SLOT = [4, 5, 6, 7]
 
+GROUPS = [[(u, 0, H)] for u in range(UNITS)]
+SHARE_W = [0, 0, 0, 0, 0, 0, 224, 224, 192, 192, 192, 192]
+LOADS = ["zscale","z0","w0","z0.0","w0.0","z0.1","w0.1","z0.2","w0.2","z0.3","w0.3","z1","w1","z2","h","gs","bias","w2","z3","w3","c","z4","w4","z5","w5"]
+LATER = ["z6", "w6", "z7", "w7", "z8", "w8", "z9", "w9", "z10", "w10", "cgs", "z11", "w11"]
+LOADS_PER_STAGE = 2
+RAWBUFS = 6
+WIDEBUFS = 4
+WORKBUFS = 4
+CODEBUFS = 4
+LEAD = 2
+LEADW = 1
+LATE = 1
+TURN_H = 0
+QUANT_H = 1
+TURN_C = 2
+FC_PER_STAGE = 1
+RG1_PER_STAGE = 2
+CELL_AFTER = 3
+TANH_AFTER = 4
+RG2_SPLIT = 3
+EARLY_OUT = 104
+SIG_FIRST = False
+SIG_LIMIT = 8
+FC_AFTER = 1
+FLUSH_AT = [10]
+HT_N = 1
+QZ_EARLY = True
+Z_BY_PLANE = [0]
+W_CHUNKS = {0: 4}
+Q_PIECES = {11: 4}
+END_STEP = 4
+HEAD_EXTRA = 1
+AFFINE_ON_S = False
+TANH_LAST = False
+WEAVE_AFTER = [3]
+
+NG = len(GROUPS)
 FLOPS = 2 * (B * NB + B) * H * H * GH * T
 
 
@@ -32,8 +65,9 @@ def tile_st_hmr_pc_kernel(tc, h_new, c_new, g_s, c_g_s, Wg_s, Zg_s_bytes, Zg_s_s
     with ExitStack() as ctx:
         const = ctx.enter_context(tc.tile_pool(name="const", bufs=1))
         raw = ctx.enter_context(tc.tile_pool(name="raw", bufs=RAWBUFS))
-        work = ctx.enter_context(tc.tile_pool(name="work", bufs=4))
-        codes = ctx.enter_context(tc.tile_pool(name="codes", bufs=4))
+        wide = ctx.enter_context(tc.tile_pool(name="wide", bufs=WIDEBUFS))
+        work = ctx.enter_context(tc.tile_pool(name="work", bufs=WORKBUFS))
+        codes = ctx.enter_context(tc.tile_pool(name="codes", bufs=CODEBUFS))
         mxps = ctx.enter_context(tc.psum_pool(name="mxps", bufs=4))
         aux = ctx.enter_context(tc.psum_pool(name="aux", bufs=4))
         ctx.enter_context(tc.manual_schedule())
@@ -71,11 +105,10 @@ def tile_st_hmr_pc_kernel(tc, h_new, c_new, g_s, c_g_s, Wg_s, Zg_s_bytes, Zg_s_s
         gnew = const.tile([P, H], F32, name="gnew")
         gate_a = {}
         gate_b = {}
-        last = {}
         for ft in range(FT):
             gate_a[ft] = const.tile([P, NB, T, B], F32, name="gate_a%d" % ft)
             gate_b[ft] = const.tile([P, NB, T, B], F32, name="gate_b%d" % ft)
-            last[ft] = const.tile([P, NB, B], F32, name="last%d" % ft)
+        last = const.tile([P, FT, NB, LATE, B], F32, name="last")
 
         zbytes = {}
         wraw = {}
@@ -87,73 +120,132 @@ def tile_st_hmr_pc_kernel(tc, h_new, c_new, g_s, c_g_s, Wg_s, Zg_s_bytes, Zg_s_s
         mxp = {}
         cT = {}
         acc = {}
+        width = [sum(c1 - c0 for (u, c0, c1) in grp) for grp in GROUPS]
+        st = {}
+        for g in range(NG):
+            for (u, c0, c1) in GROUPS[g]:
+                st[u] = g
 
-        def load_z(u):
-            zbytes[u] = raw.tile([P, 4, H], U8, name="zbytes", tag="zbytes")
-            nc.sync.dma_start(out=zbytes[u][:], in_=Zg_s_bytes[u // T, u % T].rearrange("(p j) n -> p j n", j=4))
+        def load_z(g):
+            zbytes[g] = raw.tile([P, 4, width[g]], U8, name="zbytes", tag="zbytes")
+            o = 0
+            for (u, c0, c1) in GROUPS[g]:
+                src = Zg_s_bytes[u // T, u % T].rearrange("(p j) n -> p j n", j=4)
+                if g in Z_BY_PLANE:
+                    continue
+                nc.sync.dma_start(out=zbytes[g][:, :, o:o + c1 - c0], in_=src[:, :, c0:c1])
+                o += c1 - c0
 
-        def load_w(u):
-            wraw[u] = raw.tile([P, 4, H], BF16, name="wraw", tag="wraw")
-            nc.sync.dma_start(out=wraw[u][:], in_=Wg_s[u // T, u % T].rearrange("(p j) n -> p j n", j=4))
+        def load_z_plane(g, j):
+            (u, c0, c1) = GROUPS[g][0]
+            src = Zg_s_bytes[u // T, u % T].rearrange("(p j) n -> p j n", j=4)
+            nc.sync.dma_start(out=zbytes[g][:, j, :], in_=src[:, j, c0:c1])
 
-        def widen(u):
-            zwide[u] = work.tile([P, 4, H], BF16, name="zwide", tag="zwide")
+        def load_w(g):
+            wraw[g] = raw.tile([P, 4, width[g]], BF16, name="wraw", tag="wraw")
+            o = 0
+            for (u, c0, c1) in GROUPS[g]:
+                if g in W_CHUNKS:
+                    continue
+                nc.sync.dma_start(out=wraw[g][:, :, o:o + c1 - c0],
+                                  in_=Wg_s[u // T, u % T].rearrange("(p j) n -> p j n", j=4)[:, :, c0:c1])
+                o += c1 - c0
+
+        def load_w_chunk(g, k):
+            (u, c0, c1) = GROUPS[g][0]
+            w = (c1 - c0) // W_CHUNKS[g]
+            nc.sync.dma_start(out=wraw[g][:, :, k * w:(k + 1) * w],
+                              in_=Wg_s[u // T, u % T].rearrange("(p j) n -> p j n", j=4)[:, :, c0 + k * w:c0 + (k + 1) * w])
+
+        def widen(g):
+            zwide[g] = wide.tile([P, 4, width[g]], BF16, name="zwide", tag="zwide")
             for j in range(4):
-                nc.scalar.activation(out=zwide[u][:, j, :], in_=zbytes[u][:, j, :].bitcast(FP8), func=ACT.Copy,
+                nc.scalar.activation(out=zwide[g][:, j, :], in_=zbytes[g][:, j, :].bitcast(FP8), func=ACT.Copy,
                                      scale=zscale[:, j:j + 1])
 
-        def wil_tile(u):
-            if u not in wil:
-                wil[u] = work.tile([P, H, 4], BF16, name="wil", tag="wil", align_bytes=64)
-            return wil[u]
+        def wil_tile(g):
+            if g not in wil:
+                wil[g] = work.tile([P, width[g], 4], BF16, name="wil", tag="wil", align_bytes=64)
+            return wil[g]
 
-        def il_w_scalar(u):
-            c0 = H - SHARE_W[u]
-            if c0 < H:
-                nc.scalar.copy(out=wil_tile(u)[:, c0:H, :].rearrange("p (g i) j -> p g j i", i=4),
-                               in_=wraw[u][:, :, c0:H].rearrange("p j (g i) -> p g j i", i=4))
+        def il_w_scalar(g):
+            c0 = width[g] - SHARE_W[g]
+            if c0 < width[g]:
+                nc.scalar.copy(out=wil_tile(g)[:, c0:width[g], :].rearrange("p (g i) j -> p g j i", i=4),
+                               in_=wraw[g][:, :, c0:width[g]].rearrange("p j (g i) -> p g j i", i=4))
 
-        def il_w(u):
-            c0 = H - SHARE_W[u]
-            nc.vector.tensor_copy(out=wil_tile(u)[:, 0:c0, :].rearrange("p (g i) j -> p g j i", i=4),
-                                  in_=wraw[u][:, :, 0:c0].rearrange("p j (g i) -> p g j i", i=4))
+        def il_w(g):
+            c0 = width[g] - SHARE_W[g]
+            n = W_CHUNKS.get(g, 1)
+            for k in range(n):
+                a, b = k * c0 // n, (k + 1) * c0 // n
+                nc.vector.tensor_copy(out=wil_tile(g)[:, a:b, :].rearrange("p (g i) j -> p g j i", i=4),
+                                      in_=wraw[g][:, :, a:b].rearrange("p j (g i) -> p g j i", i=4))
 
-        def il_z(u):
-            zil[u] = work.tile([P, H, 4], BF16, name="zil", tag="zil", align_bytes=64)
-            nc.vector.tensor_copy(out=zil[u][:].rearrange("p (g i) j -> p g j i", i=4),
-                                  in_=zwide[u][:].rearrange("p j (g i) -> p g j i", i=4))
+        def il_z(g):
+            zil[g] = work.tile([P, width[g], 4], BF16, name="zil", tag="zil", align_bytes=64)
+            nc.vector.tensor_copy(out=zil[g][:].rearrange("p (g i) j -> p g j i", i=4),
+                                  in_=zwide[g][:].rearrange("p j (g i) -> p g j i", i=4))
 
-        def quant(src, store, u, nm):
-            q = codes.tile([P, H], U32, name=nm + "q", tag=nm + "q", align_bytes=64)
-            s = codes.tile([P, H], U8, name=nm + "s", tag=nm + "s", align_bytes=64)
-            nc.vector.quantize_mx(out=q[:].bitcast(FP8X4), scales=s[:], in_=src[u][:].rearrange("p c j -> p (c j)"))
-            store[u] = (q, s)
+        def quant(src, store, g, nm, a=0, b=None):
+            if a == 0:
+                q = codes.tile([P, width[g]], U32, name=nm + "q", tag=nm + "q", align_bytes=64)
+                s = codes.tile([P, width[g]], U8, name=nm + "s", tag=nm + "s", align_bytes=64)
+                store[g] = (q, s)
+            q, s = store[g]
+            if b is None:
+                b = width[g]
+            nc.vector.quantize_mx(out=q[:, a:b].bitcast(FP8X4), scales=s[:, a:b],
+                                  in_=src[g][:, a:b, :].rearrange("p c j -> p (c j)"))
 
-        def mm(u):
-            t = u % T
-            cols = slice(t * COLS, (t + 1) * COLS)
-            for ft in range(FT):
-                if ft % 2 == 0:
-                    mxp[(u, ft // 2)] = mxps.tile([P, 2, COLS], F32, name="mxp", tag="mxp")
-                ps = mxp[(u, ft // 2)][:, ft % 2, :]
-                fs = slice(ft * P, (ft + 1) * P)
-                nc.tensor.matmul_mx(out=ps, lhsT=wq[u][0][:, fs].bitcast(FP8X4), lhsT_scale=wq[u][1][:, fs],
-                                    rhs=hq[:, cols].bitcast(FP8X4), rhs_scale=hs[:, cols], start=True, stop=False)
-                nc.tensor.matmul_mx(out=ps, lhsT=zq[u][0][:, fs].bitcast(FP8X4), lhsT_scale=zq[u][1][:, fs],
-                                    rhs=gq[:, cols].bitcast(FP8X4), rhs_scale=gsc[:, cols], start=False, stop=True)
+        pend = []
 
-        def sig(u):
+        def mm(g, only=None):
+            o = 0
+            for (u, c0, c1) in GROUPS[g]:
+                t = u % T
+                cols = slice(t * COLS, (t + 1) * COLS)
+                for ft in range(c0 // P, c1 // P):
+                    if only is not None and ft not in only:
+                        continue
+                    if g in Q_PIECES:
+                        mxp[(u, ft)] = mxps.tile([P, COLS], F32, name="mxp", tag="mxp")
+                        ps = mxp[(u, ft)][:]
+                    else:
+                        if ft % 2 == 0:
+                            mxp[(u, ft // 2)] = mxps.tile([P, 2, COLS], F32, name="mxp", tag="mxp")
+                        ps = mxp[(u, ft // 2)][:, ft % 2, :]
+                    fs = slice(o + ft * P - c0, o + (ft + 1) * P - c0)
+                    nc.tensor.matmul_mx(out=ps, lhsT=wq[g][0][:, fs].bitcast(FP8X4), lhsT_scale=wq[g][1][:, fs],
+                                        rhs=hq[:, cols].bitcast(FP8X4), rhs_scale=hs[:, cols], start=True, stop=False)
+                    nc.tensor.matmul_mx(out=ps, lhsT=zq[g][0][:, fs].bitcast(FP8X4), lhsT_scale=zq[g][1][:, fs],
+                                        rhs=gq[:, cols].bitcast(FP8X4), rhs_scale=gsc[:, cols], start=False, stop=True)
+                    pend.append((u, ft))
+                o += c1 - c0
+
+        def sig(u, ft):
             g, t = u // T, u % T
-            for ft in range(FT):
-                if u == UNITS - 1:
-                    dst = last[ft][:]
-                elif g == 1:
-                    dst = gate_b[ft][:, :, t, :]
-                else:
-                    dst = gate_a[ft][:, :, t, :]
-                col = u * FT + ft
-                nc.scalar.activation(out=dst, in_=mxp[(u, ft // 2)][:, ft % 2, :].rearrange("p (n b) -> p n b", b=B),
-                                     func=ACT.Sigmoid, bias=bias_sb[:, col:col + 1], scale=1.0)
+            if u >= UNITS - LATE:
+                dst = last[:, ft, :, u - (UNITS - LATE), :]
+            elif g == 1:
+                dst = gate_b[ft][:, :, t, :]
+            else:
+                dst = gate_a[ft][:, :, t, :]
+            col = u * FT + ft
+            src = mxp[(u, ft)][:] if st[u] in Q_PIECES else mxp[(u, ft // 2)][:, ft % 2, :]
+            nc.scalar.activation(out=dst, in_=src.rearrange("p (n b) -> p n b", b=B),
+                                 func=ACT.Sigmoid, bias=bias_sb[:, col:col + 1], scale=1.0)
+
+        rg2 = []
+
+        def sigs(limit):
+            for k in range(min(limit, len(pend))):
+                u, ft = pend.pop(0)
+                sig(u, ft)
+                if u == UNITS - LATE - 1 and ft == FT - 1:
+                    for f2 in range(RG2_SPLIT):
+                        reduce_gate(2, f2)
+                    rg2.extend(range(RG2_SPLIT, FT))
 
         def reduce_gate(g, ft):
             if ft == 0:
@@ -163,123 +255,184 @@ def tile_st_hmr_pc_kernel(tc, h_new, c_new, g_s, c_g_s, Wg_s, Zg_s_bytes, Zg_s_s
                 nc.tensor.matmul(out=acc[g][:, ft * P:(ft + 1) * P], lhsT=src[:, n].rearrange("p t b -> p (t b)"),
                                  rhs=ident_f[:], is_transpose=True, start=(n == 0), stop=(n == NB - 1))
 
-        nc.sync.dma_start(out=zscale[:], in_=Zg_s_scale[0, 0].rearrange("(p j) c -> p (j c)", j=4))
-        load_z(0)
-        load_w(0)
-        load_z(1)
-        load_w(1)
-        nc.sync.dma_start(out=h_sb[:], in_=h_new.rearrange("b t n h -> (b t) n h"))
-        nc.sync.dma_start(out=gs_sb[:], in_=g_s.rearrange("b t h -> (b t) h"))
-        nc.sync.dma_start(out=bias_raw[0:UNITS * FT, :], in_=bg_s.rearrange("g t o (c f) -> (g t o c) f", f=P))
-        load_z(2)
-        load_w(2)
-        load_z(3)
-        load_w(3)
-        nc.sync.dma_start(out=c_sb[:], in_=c_new.rearrange("b t n h -> (b t) n h"))
-        for u in range(4, RAWBUFS):
-            load_z(u)
-            load_w(u)
-
-        for u in range(LEAD):
-            widen(u)
-        il_w_scalar(0)
-        il_w(0)
-
-        hin_w = hin[:].bitcast(F32).rearrange("p (t n b u) -> p t n b u", t=T, n=NB, b=B, u=2)
-        next_sig = 0
-        issued_mm = 0
-        for i in range(UNITS + 1):
-            if i == 0:
-                hw = h_sb[:].bitcast(F32)
-                hT = None
-                for n in range(NB):
-                    hT = aux.tile([P, 2, P], F32, name="hT", tag="aux")
-                    for u in range(2):
-                        nc.tensor.transpose(hT[:, u, :], hw[:, n, u::2], ident_f[:])
-                    nc.scalar.copy(out=hin_w[:, :, n, :, :], in_=hT[:].rearrange("p u (b t) -> p t b u", t=T))
-                gw = gs_sb[:].bitcast(F32)
-                gT = aux.tile([P, 2, P], F32, name="gT", tag="aux")
-                for u in range(2):
-                    nc.tensor.transpose(gT[:, u, :], gw[:, u::2], ident_f[:])
-                bT = aux.tile([P, P], BF16, name="bT", tag="aux")
-                nc.tensor.transpose(bT[:], bias_raw[:], ident_b[:])
-                nc.scalar.copy(out=gin0[:].bitcast(F32).rearrange("p (t b u) -> p t b u", t=T, b=B, u=2),
-                               in_=gT[:].rearrange("p u (b t) -> p t b u", t=T))
-            if i + LEAD < UNITS:
-                widen(i + LEAD)
-            if i + 1 < UNITS:
-                il_w_scalar(i + 1)
-            for k in range(min(2, issued_mm - next_sig)):
-                sig(next_sig)
-                next_sig += 1
-            if i == UNITS - 1:
-                nc.scalar.activation(out=s2[:], in_=cnew[:], func=ACT.Sigmoid, scale=2.0)
-            if i < UNITS:
-                il_z(i)
-                quant(wil, wq, i, "w")
-            if i + 1 < UNITS:
-                il_w(i + 1)
-            if i < UNITS:
-                quant(zil, zq, i, "z")
-            if i == 1:
-                nc.vector.tensor_copy(out=bias_sb[:], in_=bT[:, 0:UNITS * FT])
-                nc.vector.quantize_mx(out=hq[:].bitcast(FP8X4), scales=hs[:], in_=hin[:])
-                nc.vector.quantize_mx(out=gq0[:].bitcast(FP8X4), scales=gs0[:], in_=gin0[:])
-                nc.vector.tensor_copy(
-                    out=gq[:].bitcast(I32).rearrange("p (t n b) -> p t n b", t=T, n=NB, b=B),
-                    in_=gq0[:].bitcast(I32).rearrange("p (t b) -> p t b", t=T).unsqueeze(2).to_broadcast([P, T, NB, B]))
-                nc.vector.tensor_copy(
-                    out=gsc[:].bitcast(I32).rearrange("p (t n w) -> p t n w", t=T, n=NB, w=B // 4),
-                    in_=gs0[:].bitcast(I32).rearrange("p (t w) -> p t w", t=T).unsqueeze(2).to_broadcast(
-                        [P, T, NB, B // 4]))
-                mm(0)
-                issued_mm += 1
-            if 1 <= i < UNITS:
-                mm(i)
-                issued_mm += 1
-            if i == 2:
-                for ft in range(FT):
-                    cT[ft] = aux.tile([P, NB, P], BF16, name="cT", tag="aux")
-                    for n in range(NB):
-                        nc.tensor.transpose(cT[ft][:, n, :], c_sb[:, n, ft * P:(ft + 1) * P], ident_b[:])
-            for ft in range(FT):
-                if FC_SLOT[ft] == i:
-                    f = gate_a[ft]
-                    nc.vector.tensor_tensor(out=f[:], in0=f[:], in1=cT[ft][:].rearrange("p n (b t) -> p n t b", t=T),
-                                            op=ALU.mult)
-                    reduce_gate(0, ft)
-            if i == 8:
-                reduce_gate(1, 0)
-                reduce_gate(1, 1)
-            if i == 9:
-                reduce_gate(1, 2)
-                reduce_gate(1, 3)
-            if i == 10:
-                nc.vector.scalar_tensor_tensor(out=t1[:], in0=acc[1][:], scalar=0.125, in1=cgs[:], op0=ALU.mult,
-                                               op1=ALU.mult)
-                nc.vector.scalar_tensor_tensor(out=cnew[:], in0=acc[0][:], scalar=0.125, in1=t1[:], op0=ALU.mult,
-                                               op1=ALU.add)
-                for t in range(T):
-                    nc.sync.dma_start(out=out_1[:, t, :], in_=cnew[t * B:(t + 1) * B, :])
-                sig(next_sig)
-                next_sig += 1
-                for ft in range(FT):
-                    reduce_gate(2, ft)
-            if i + RAWBUFS < UNITS:
-                load_z(i + RAWBUFS)
-                load_w(i + RAWBUFS)
-            if i == 4:
+        def load_named(what):
+            if what == "zscale":
+                nc.sync.dma_start(out=zscale[:], in_=Zg_s_scale[0, 0].rearrange("(p j) c -> p (j c)", j=4))
+            elif what == "h":
+                nc.sync.dma_start(out=h_sb[:], in_=h_new.rearrange("b t n h -> (b t) n h"))
+            elif what == "gs":
+                nc.sync.dma_start(out=gs_sb[:], in_=g_s.rearrange("b t h -> (b t) h"))
+            elif what == "bias":
+                nc.sync.dma_start(out=bias_raw[0:UNITS * FT, :], in_=bg_s.rearrange("g t o (c f) -> (g t o c) f", f=P))
+            elif what == "c":
+                nc.sync.dma_start(out=c_sb[:], in_=c_new.rearrange("b t n h -> (b t) n h"))
+            elif what == "cgs":
                 for t in range(T):
                     nc.sync.dma_start(out=cgs[t * B:(t + 1) * B, :], in_=c_g_s[:, t, :])
+            elif what[0] == "w" and "." in what:
+                load_w_chunk(int(what[1:].split(".")[0]), int(what.split(".")[1]))
+            elif what[0] == "z" and "." in what:
+                load_z_plane(int(what[1:].split(".")[0]), int(what.split(".")[1]))
+            elif what[0] == "w":
+                load_w(int(what[1:]))
+            else:
+                load_z(int(what[1:]))
 
-        R = (T - 1) * B
-        nc.vector.tensor_scalar(out=s2[:], in0=s2[:], scalar1=0.25, scalar2=-0.125, op0=ALU.mult, op1=ALU.add)
-        nc.vector.tensor_tensor(out=gnew[0:R, :], in0=acc[2][0:R, :], in1=s2[0:R, :], op=ALU.mult)
-        for t in range(T - 1):
-            nc.sync.dma_start(out=out_0[:, t, :], in_=gnew[t * B:(t + 1) * B, :])
+        hin_w = hin[:].bitcast(F32).rearrange("p (t n b u) -> p t n b u", t=T, n=NB, b=B, u=2)
+        small = {}
+
+        def turn_h():
+            hw = h_sb[:].bitcast(F32)
+            hT = None
+            for n in range(NB):
+                if n % HT_N == 0:
+                    hT = aux.tile([P, HT_N, 2, P], F32, name="hT", tag="aux")
+                for u in range(2):
+                    nc.tensor.transpose(hT[:, n % HT_N, u, :], hw[:, n, u::2], ident_f[:])
+                nc.scalar.copy(out=hin_w[:, :, n, :, :], in_=hT[:, n % HT_N].rearrange("p u (b t) -> p t b u", t=T))
+            gw = gs_sb[:].bitcast(F32)
+            gT = aux.tile([P, 2, P], F32, name="gT", tag="aux")
+            for u in range(2):
+                nc.tensor.transpose(gT[:, u, :], gw[:, u::2], ident_f[:])
+            small["bT"] = aux.tile([P, P], BF16, name="bT", tag="aux")
+            nc.tensor.transpose(small["bT"][:], bias_raw[:], ident_b[:])
+            nc.scalar.copy(out=gin0[:].bitcast(F32).rearrange("p (t b u) -> p t b u", t=T, b=B, u=2),
+                           in_=gT[:].rearrange("p u (b t) -> p t b u", t=T))
+
+        def quant_h():
+            nc.vector.tensor_copy(out=bias_sb[:], in_=small["bT"][:, 0:UNITS * FT])
+            nc.vector.quantize_mx(out=hq[:].bitcast(FP8X4), scales=hs[:], in_=hin[:])
+            nc.vector.quantize_mx(out=gq0[:].bitcast(FP8X4), scales=gs0[:], in_=gin0[:])
+            nc.vector.tensor_copy(
+                out=gq[:].bitcast(I32).rearrange("p (t n b) -> p t n b", t=T, n=NB, b=B),
+                in_=gq0[:].bitcast(I32).rearrange("p (t b) -> p t b", t=T).unsqueeze(2).to_broadcast([P, T, NB, B]))
+            nc.vector.tensor_copy(
+                out=gsc[:].bitcast(I32).rearrange("p (t n w) -> p t n w", t=T, n=NB, w=B // 4),
+                in_=gs0[:].bitcast(I32).rearrange("p (t w) -> p t w", t=T).unsqueeze(2).to_broadcast([P, T, NB, B // 4]))
+
+        def turn_c():
+            for ft in range(FT):
+                cT[ft] = aux.tile([P, NB, P], BF16, name="cT", tag="aux")
+                for n in range(NB):
+                    nc.tensor.transpose(cT[ft][:, n, :], c_sb[:, n, ft * P:(ft + 1) * P], ident_b[:])
+
+        def f_times_c(ft):
+            f = gate_a[ft]
+            nc.vector.tensor_tensor(out=f[:], in0=f[:], in1=cT[ft][:].rearrange("p n (b t) -> p n t b", t=T), op=ALU.mult)
+            reduce_gate(0, ft)
+
+        def new_cell():
+            nc.vector.scalar_tensor_tensor(out=t1[:], in0=acc[1][:], scalar=0.125, in1=cgs[:], op0=ALU.mult, op1=ALU.mult)
+            nc.vector.scalar_tensor_tensor(out=cnew[:], in0=acc[0][:], scalar=0.125, in1=t1[:], op0=ALU.mult, op1=ALU.add)
+            for t in range(T):
+                nc.sync.dma_start(out=out_1[:, t, :], in_=cnew[t * B:(t + 1) * B, :])
+
+        def tanh_eighth():
+            nc.scalar.activation(out=s2[:], in_=cnew[:], func=ACT.Sigmoid, scale=2.0)
+            if AFFINE_ON_S:
+                nc.scalar.activation(out=s2[:], in_=s2[:], func=ACT.Copy, scale=0.25, bias=-0.125)
+
+        R = (T - LATE) * B
+
+        def early_out():
+            if not AFFINE_ON_S:
+                nc.vector.tensor_scalar(out=s2[:], in0=s2[:], scalar1=0.25, scalar2=-0.125, op0=ALU.mult, op1=ALU.add)
+            nc.vector.tensor_tensor(out=gnew[0:R, :], in0=acc[2][0:R, :], in1=s2[0:R, :], op=ALU.mult)
+            for t in range(T - LATE):
+                nc.sync.dma_start(out=out_0[:, t, :], in_=gnew[t * B:(t + 1) * B, :])
+
+        for what in LOADS:
+            load_named(what)
+        later = list(LATER)
+
+        for g in range(LEAD + HEAD_EXTRA):
+            widen(g)
+        for g in range(LEADW):
+            il_w_scalar(g)
+            il_w(g)
+
+        waiting = []
+        have_h = False
+        for s in range(NG + 1):
+            if s == TURN_H:
+                turn_h()
+            if s == st[7] + TANH_AFTER and not TANH_LAST:
+                tanh_eighth()
+            if SIG_FIRST:
+                sigs(SIG_LIMIT)
+            if s + LEAD < NG and s + LEAD not in zwide:
+                widen(s + LEAD)
+            if s + LEADW < NG:
+                il_w_scalar(s + LEADW)
+            if not SIG_FIRST:
+                sigs(SIG_LIMIT)
+            if s == st[7] + TANH_AFTER and TANH_LAST:
+                tanh_eighth()
+            if s < NG:
+                il_z(s)
+            if s < NG and s not in Q_PIECES:
+                quant(wil, wq, s, "w")
+            if s + LEADW < NG and not QZ_EARLY:
+                il_w(s + LEADW)
+            if s == EARLY_OUT:
+                early_out()
+            if s < NG and s not in Q_PIECES:
+                quant(zil, zq, s, "z")
+                waiting.append(s)
+            if s in Q_PIECES:
+                n = Q_PIECES[s]
+                w = width[s] // n
+                for k in range(n):
+                    quant(wil, wq, s, "w", k * w, (k + 1) * w)
+                    quant(zil, zq, s, "z", k * w, (k + 1) * w)
+                    mm(s, only=list(range(k * w // P, (k + 1) * w // P)))
+                    if k in WEAVE_AFTER and rg2:
+                        reduce_gate(2, rg2[0])
+                        rg2.remove(rg2[0])
+            if s + LEADW < NG and QZ_EARLY:
+                il_w(s + LEADW)
+            if s == QUANT_H:
+                quant_h()
+                have_h = True
+            if have_h:
+                for g in waiting:
+                    mm(g)
+                waiting = []
+            if s == TURN_C:
+                turn_c()
+            for ft in range(FT):
+                if st[3] + FC_AFTER + ft // FC_PER_STAGE == s:
+                    f_times_c(ft)
+            for ft in range(FT):
+                if st[7] + 1 + ft // RG1_PER_STAGE == s:
+                    reduce_gate(1, ft)
+            if s == st[7] + CELL_AFTER:
+                new_cell()
+            for ft in rg2:
+                reduce_gate(2, ft)
+            rg2.clear()
+            if s in FLUSH_AT:
+                sigs(99)
+            for k in range(LOADS_PER_STAGE):
+                if later:
+                    load_named(later.pop(0))
+
+        if EARLY_OUT == 99:
+            early_out()
+        for k in range(LATE - 1):
+            nc.vector.tensor_reduce(out=r3[:, :, R + k * B:R + (k + 1) * B],
+                                    in_=last[:, :, :, k, :].rearrange("p f n b -> p f b n"), axis=AX.X, op=ALU.add)
         acc3 = aux.tile([P, H], F32, name="acc3", tag="aux")
         for ft in range(FT):
-            nc.vector.tensor_reduce(out=r3[:, ft, R:P], in_=last[ft][:].rearrange("p n b -> p b n"), axis=AX.X, op=ALU.add)
+            if ft == EARLY_OUT - 100:
+                early_out()
+            nc.vector.tensor_reduce(out=r3[:, ft, P - B:P], in_=last[:, ft, :, LATE - 1, :].rearrange("p n b -> p b n"),
+                                    axis=AX.X, op=ALU.add)
             nc.tensor.transpose(acc3[:, ft * P:(ft + 1) * P], r3[:, ft, :], ident_f[:])
-        nc.vector.tensor_tensor(out=gnew[R:P, :], in0=acc3[R:P, :], in1=s2[R:P, :], op=ALU.mult)
-        nc.sync.dma_start(out=out_0[:, T - 1, :], in_=gnew[R:P, :])
+            if ft == FT - 1 and EARLY_OUT == 104:
+                early_out()
+            if (ft + 1) % END_STEP == 0:
+                fs = slice((ft + 1 - END_STEP) * P, (ft + 1) * P)
+                nc.vector.tensor_tensor(out=gnew[R:P, fs], in0=acc3[R:P, fs], in1=s2[R:P, fs], op=ALU.mult)
+        for t in range(T - LATE, T):
+            nc.sync.dma_start(out=out_0[:, t, :], in_=gnew[t * B:(t + 1) * B, :])

@@ -21,7 +21,7 @@ UNITS = GH * T
 COLS = NB * B
 
 GROUPS = [[(u, 0, H)] for u in range(UNITS)]
-SHARE_W = [0, 0, 0, 0, 0, 0, 224, 224, 192, 192, 192, 192]
+SHARE_W = [0, 0, 0, 0, 0, 0, 224, 160, 128, 128, 128, 192]
 LOADS = ["zscale","z0","w0","z0.0","w0.0","z0.1","w0.1","z0.2","w0.2","z0.3","w0.3","z1","w1","z2","h","gs","bias","w2","z3","w3","c","z4","w4","z5","w5"]
 LATER = ["z6", "w6", "z7", "w7", "z8", "w8", "z9", "w9", "z10", "w10", "cgs", "z11", "w11"]
 LOADS_PER_STAGE = 2
@@ -43,7 +43,7 @@ RG2_SPLIT = 3
 EARLY_OUT = 104
 SIG_FIRST = False
 SIG_LIMIT = 8
-FC_AFTER = 1
+FC_AFTER = 2
 FLUSH_AT = [10]
 HT_N = 1
 QZ_EARLY = True
@@ -52,9 +52,12 @@ W_CHUNKS = {0: 4}
 Q_PIECES = {11: 4}
 END_STEP = 4
 HEAD_EXTRA = 1
-AFFINE_ON_S = False
+AFFINE_ON_S = True
 TANH_LAST = False
 WEAVE_AFTER = [3]
+WILBUFS = 2
+SHARE_G = [0, 0, 0, 0, 0, 0, 0, 152, 152, 152, 152, 0]
+FC_EARLY = True
 
 NG = len(GROUPS)
 FLOPS = 2 * (B * NB + B) * H * H * GH * T
@@ -67,6 +70,7 @@ def tile_st_hmr_pc_kernel(tc, h_new, c_new, g_s, c_g_s, Wg_s, Zg_s_bytes, Zg_s_s
         raw = ctx.enter_context(tc.tile_pool(name="raw", bufs=RAWBUFS))
         wide = ctx.enter_context(tc.tile_pool(name="wide", bufs=WIDEBUFS))
         work = ctx.enter_context(tc.tile_pool(name="work", bufs=WORKBUFS))
+        wpool = ctx.enter_context(tc.tile_pool(name="wpool", bufs=WILBUFS))
         codes = ctx.enter_context(tc.tile_pool(name="codes", bufs=CODEBUFS))
         mxps = ctx.enter_context(tc.psum_pool(name="mxps", bufs=4))
         aux = ctx.enter_context(tc.psum_pool(name="aux", bufs=4))
@@ -165,7 +169,7 @@ def tile_st_hmr_pc_kernel(tc, h_new, c_new, g_s, c_g_s, Wg_s, Zg_s_bytes, Zg_s_s
 
         def wil_tile(g):
             if g not in wil:
-                wil[g] = work.tile([P, width[g], 4], BF16, name="wil", tag="wil", align_bytes=64)
+                wil[g] = wpool.tile([P, width[g], 4], BF16, name="wil", tag="wil", align_bytes=64)
             return wil[g]
 
         def il_w_scalar(g):
@@ -174,8 +178,16 @@ def tile_st_hmr_pc_kernel(tc, h_new, c_new, g_s, c_g_s, Wg_s, Zg_s_bytes, Zg_s_s
                 nc.scalar.copy(out=wil_tile(g)[:, c0:width[g], :].rearrange("p (g i) j -> p g j i", i=4),
                                in_=wraw[g][:, :, c0:width[g]].rearrange("p j (g i) -> p g j i", i=4))
 
+        def il_w_gpsimd(g):
+            b = width[g] - SHARE_W[g]
+            a = b - SHARE_G[g]
+            if a < b:
+                nc.gpsimd.tensor_scalar(out=wil_tile(g)[:, a:b, :].rearrange("p (g i) j -> p g j i", i=4),
+                                        in0=wraw[g][:, :, a:b].rearrange("p j (g i) -> p g j i", i=4),
+                                        scalar1=1.0, scalar2=0.0, op0=ALU.mult, op1=ALU.add)
+
         def il_w(g):
-            c0 = width[g] - SHARE_W[g]
+            c0 = width[g] - SHARE_W[g] - SHARE_G[g]
             n = W_CHUNKS.get(g, 1)
             for k in range(n):
                 a, b = k * c0 // n, (k + 1) * c0 // n
@@ -372,6 +384,12 @@ def tile_st_hmr_pc_kernel(tc, h_new, c_new, g_s, c_g_s, Wg_s, Zg_s_bytes, Zg_s_s
                 il_z(s)
             if s < NG and s not in Q_PIECES:
                 quant(wil, wq, s, "w")
+            if FC_EARLY:
+                for ft in range(FT):
+                    if st[3] + FC_AFTER + ft // FC_PER_STAGE == s:
+                        f_times_c(ft)
+                if s + 2 < NG:
+                    il_w_gpsimd(s + 2)
             if s + LEADW < NG and not QZ_EARLY:
                 il_w(s + LEADW)
             if s == EARLY_OUT:
@@ -401,7 +419,7 @@ def tile_st_hmr_pc_kernel(tc, h_new, c_new, g_s, c_g_s, Wg_s, Zg_s_bytes, Zg_s_s
             if s == TURN_C:
                 turn_c()
             for ft in range(FT):
-                if st[3] + FC_AFTER + ft // FC_PER_STAGE == s:
+                if st[3] + FC_AFTER + ft // FC_PER_STAGE == s and not FC_EARLY:
                     f_times_c(ft)
             for ft in range(FT):
                 if st[7] + 1 + ft // RG1_PER_STAGE == s:

@@ -21,7 +21,7 @@ UNITS = GH * T
 COLS = NB * B
 
 GROUPS = [[(u, 0, H)] for u in range(UNITS)]
-SHARE_W = [0, 0, 0, 0, 0, 0, 224, 160, 128, 128, 128, 192]
+SHARE_W = [0, 0, 0, 0, 0, 0, 160, 96, 64, 64, 64, 128]
 LOADS = ["zscale","z0","w0","z0.0","w0.0","z0.1","w0.1","z0.2","w0.2","z0.3","w0.3","z1","w1","z2","h","gs","bias","w2","z3","w3","c","z4","w4","z5","w5"]
 LATER = ["z6", "w6", "z7", "w7", "z8", "w8", "z9", "w9", "z10", "w10", "cgs", "z11", "w11"]
 LOADS_PER_STAGE = 2
@@ -58,6 +58,10 @@ WEAVE_AFTER = [3]
 WILBUFS = 2
 SHARE_G = [0, 0, 0, 0, 0, 0, 0, 152, 152, 152, 152, 0]
 FC_EARLY = True
+REPL_DMA = False
+QW_FIRST = []
+IL_FORM = "runs"
+IL_RUN = 4
 
 NG = len(GROUPS)
 FLOPS = 2 * (B * NB + B) * H * H * GH * T
@@ -167,6 +171,13 @@ def tile_st_hmr_pc_kernel(tc, h_new, c_new, g_s, c_g_s, Wg_s, Zg_s_bytes, Zg_s_s
                 nc.scalar.activation(out=zwide[g][:, j, :], in_=zbytes[g][:, j, :].bitcast(FP8), func=ACT.Copy,
                                      scale=zscale[:, j:j + 1])
 
+        def v_il(dst, src):
+            if IL_FORM == "halves":
+                nc.vector.tensor_copy(out=dst.rearrange("p c (h j) -> p h c j", h=2), in_=src.rearrange("p (h j) c -> p h c j", h=2))
+            else:
+                nc.vector.tensor_copy(out=dst.rearrange("p (g i) j -> p g j i", i=IL_RUN),
+                                      in_=src.rearrange("p j (g i) -> p g j i", i=IL_RUN))
+
         def wil_tile(g):
             if g not in wil:
                 wil[g] = wpool.tile([P, width[g], 4], BF16, name="wil", tag="wil", align_bytes=64)
@@ -191,13 +202,11 @@ def tile_st_hmr_pc_kernel(tc, h_new, c_new, g_s, c_g_s, Wg_s, Zg_s_bytes, Zg_s_s
             n = W_CHUNKS.get(g, 1)
             for k in range(n):
                 a, b = k * c0 // n, (k + 1) * c0 // n
-                nc.vector.tensor_copy(out=wil_tile(g)[:, a:b, :].rearrange("p (g i) j -> p g j i", i=4),
-                                      in_=wraw[g][:, :, a:b].rearrange("p j (g i) -> p g j i", i=4))
+                v_il(wil_tile(g)[:, a:b, :], wraw[g][:, :, a:b])
 
         def il_z(g):
             zil[g] = work.tile([P, width[g], 4], BF16, name="zil", tag="zil", align_bytes=64)
-            nc.vector.tensor_copy(out=zil[g][:].rearrange("p (g i) j -> p g j i", i=4),
-                                  in_=zwide[g][:].rearrange("p j (g i) -> p g j i", i=4))
+            v_il(zil[g][:], zwide[g][:])
 
         def quant(src, store, g, nm, a=0, b=None):
             if a == 0:
@@ -315,12 +324,19 @@ def tile_st_hmr_pc_kernel(tc, h_new, c_new, g_s, c_g_s, Wg_s, Zg_s_bytes, Zg_s_s
             nc.vector.tensor_copy(out=bias_sb[:], in_=small["bT"][:, 0:UNITS * FT])
             nc.vector.quantize_mx(out=hq[:].bitcast(FP8X4), scales=hs[:], in_=hin[:])
             nc.vector.quantize_mx(out=gq0[:].bitcast(FP8X4), scales=gs0[:], in_=gin0[:])
-            nc.vector.tensor_copy(
-                out=gq[:].bitcast(I32).rearrange("p (t n b) -> p t n b", t=T, n=NB, b=B),
-                in_=gq0[:].bitcast(I32).rearrange("p (t b) -> p t b", t=T).unsqueeze(2).to_broadcast([P, T, NB, B]))
-            nc.vector.tensor_copy(
-                out=gsc[:].bitcast(I32).rearrange("p (t n w) -> p t n w", t=T, n=NB, w=B // 4),
-                in_=gs0[:].bitcast(I32).rearrange("p (t w) -> p t w", t=T).unsqueeze(2).to_broadcast([P, T, NB, B // 4]))
+            if REPL_DMA:
+                for n in range(NB):
+                    nc.sync.dma_start(out=gq[:].bitcast(I32).rearrange("p (t n b) -> p t n b", t=T, n=NB, b=B)[:, :, n, :],
+                                      in_=gq0[:].bitcast(I32).rearrange("p (t b) -> p t b", t=T))
+                    nc.sync.dma_start(out=gsc[:].bitcast(I32).rearrange("p (t n w) -> p t n w", t=T, n=NB, w=B // 4)[:, :, n, :],
+                                      in_=gs0[:].bitcast(I32).rearrange("p (t w) -> p t w", t=T))
+            else:
+                nc.vector.tensor_copy(
+                    out=gq[:].bitcast(I32).rearrange("p (t n b) -> p t n b", t=T, n=NB, b=B),
+                    in_=gq0[:].bitcast(I32).rearrange("p (t b) -> p t b", t=T).unsqueeze(2).to_broadcast([P, T, NB, B]))
+                nc.vector.tensor_copy(
+                    out=gsc[:].bitcast(I32).rearrange("p (t n w) -> p t n w", t=T, n=NB, w=B // 4),
+                    in_=gs0[:].bitcast(I32).rearrange("p (t w) -> p t w", t=T).unsqueeze(2).to_broadcast([P, T, NB, B // 4]))
 
         def turn_c():
             for ft in range(FT):
@@ -380,9 +396,11 @@ def tile_st_hmr_pc_kernel(tc, h_new, c_new, g_s, c_g_s, Wg_s, Zg_s_bytes, Zg_s_s
                 sigs(SIG_LIMIT)
             if s == st[7] + TANH_AFTER and TANH_LAST:
                 tanh_eighth()
+            if s in QW_FIRST:
+                quant(wil, wq, s, "w")
             if s < NG:
                 il_z(s)
-            if s < NG and s not in Q_PIECES:
+            if s < NG and s not in Q_PIECES and s not in QW_FIRST:
                 quant(wil, wq, s, "w")
             if FC_EARLY:
                 for ft in range(FT):

@@ -62,6 +62,16 @@ REPL_DMA = False
 QW_FIRST = []
 IL_FORM = "runs"
 IL_RUN = 4
+ZILBUFS = 4
+SHARE_GZ = [0] * 12
+FC_SLOTS = [(5, "A"), (6, "A"), (7, "A"), (8, "A")]
+CELL_SLOT = -1
+ZGROUPS = [[g] for g in range(12)]
+SIG_FIRST_FROM = 99
+RG1_NOW = 0
+CELL_BEHIND_ILZ = -1
+WIDEN_ON_V = []
+PIN_ALL = False
 
 NG = len(GROUPS)
 FLOPS = 2 * (B * NB + B) * H * H * GH * T
@@ -75,10 +85,15 @@ def tile_st_hmr_pc_kernel(tc, h_new, c_new, g_s, c_g_s, Wg_s, Zg_s_bytes, Zg_s_s
         wide = ctx.enter_context(tc.tile_pool(name="wide", bufs=WIDEBUFS))
         work = ctx.enter_context(tc.tile_pool(name="work", bufs=WORKBUFS))
         wpool = ctx.enter_context(tc.tile_pool(name="wpool", bufs=WILBUFS))
+        zpool = ctx.enter_context(tc.tile_pool(name="zpool", bufs=ZILBUFS))
         codes = ctx.enter_context(tc.tile_pool(name="codes", bufs=CODEBUFS))
         mxps = ctx.enter_context(tc.psum_pool(name="mxps", bufs=4))
         aux = ctx.enter_context(tc.psum_pool(name="aux", bufs=4))
-        ctx.enter_context(tc.manual_schedule())
+        if PIN_ALL:
+            ctx.enter_context(tc.manual_schedule())
+        else:
+            ET = mybir.EngineType
+            ctx.enter_context(tc.manual_schedule(engines={ET.DVE, ET.Activation, ET.Pool, ET.SP}))
 
         warm = const.tile([P, 1], F32, name="warm")
         nc.vector.memset(warm[:], 0.0)
@@ -134,20 +149,29 @@ def tile_st_hmr_pc_kernel(tc, h_new, c_new, g_s, c_g_s, Wg_s, Zg_s_bytes, Zg_s_s
             for (u, c0, c1) in GROUPS[g]:
                 st[u] = g
 
-        def load_z(g):
-            zbytes[g] = raw.tile([P, 4, width[g]], U8, name="zbytes", tag="zbytes")
+        zg_of = {}
+        for k in range(len(ZGROUPS)):
             o = 0
+            for g in ZGROUPS[k]:
+                zg_of[g] = (k, o)
+                o += width[g]
+        zwidth = [sum(width[g] for g in grp) for grp in ZGROUPS]
+
+        def load_z(g):
+            k, o = zg_of[g]
+            if o == 0:
+                zbytes[k] = raw.tile([P, 4, zwidth[k]], U8, name="zbytes", tag="zbytes")
             for (u, c0, c1) in GROUPS[g]:
                 src = Zg_s_bytes[u // T, u % T].rearrange("(p j) n -> p j n", j=4)
                 if g in Z_BY_PLANE:
                     continue
-                nc.sync.dma_start(out=zbytes[g][:, :, o:o + c1 - c0], in_=src[:, :, c0:c1])
+                nc.sync.dma_start(out=zbytes[k][:, :, o:o + c1 - c0], in_=src[:, :, c0:c1])
                 o += c1 - c0
 
         def load_z_plane(g, j):
             (u, c0, c1) = GROUPS[g][0]
             src = Zg_s_bytes[u // T, u % T].rearrange("(p j) n -> p j n", j=4)
-            nc.sync.dma_start(out=zbytes[g][:, j, :], in_=src[:, j, c0:c1])
+            nc.sync.dma_start(out=zbytes[zg_of[g][0]][:, j, :], in_=src[:, j, c0:c1])
 
         def load_w(g):
             wraw[g] = raw.tile([P, 4, width[g]], BF16, name="wraw", tag="wraw")
@@ -166,10 +190,21 @@ def tile_st_hmr_pc_kernel(tc, h_new, c_new, g_s, c_g_s, Wg_s, Zg_s_bytes, Zg_s_s
                               in_=Wg_s[u // T, u % T].rearrange("(p j) n -> p j n", j=4)[:, :, c0 + k * w:c0 + (k + 1) * w])
 
         def widen(g):
-            zwide[g] = wide.tile([P, 4, width[g]], BF16, name="zwide", tag="zwide")
+            k, o = zg_of[g]
+            if k in zwide:
+                return
+            zwide[k] = wide.tile([P, 4, zwidth[k]], BF16, name="zwide", tag="zwide")
             for j in range(4):
-                nc.scalar.activation(out=zwide[g][:, j, :], in_=zbytes[g][:, j, :].bitcast(FP8), func=ACT.Copy,
+                if g in WIDEN_ON_V:
+                    nc.vector.tensor_scalar(out=zwide[k][:, j, :], in0=zbytes[k][:, j, :].bitcast(FP8), scalar1=zscale[:, j:j + 1],
+                                            scalar2=None, op0=ALU.mult)
+                    continue
+                nc.scalar.activation(out=zwide[k][:, j, :], in_=zbytes[k][:, j, :].bitcast(FP8), func=ACT.Copy,
                                      scale=zscale[:, j:j + 1])
+
+        def zwide_of(g, a, b):
+            k, o = zg_of[g]
+            return zwide[k][:, :, o + a:o + b]
 
         def v_il(dst, src):
             if IL_FORM == "halves":
@@ -204,9 +239,21 @@ def tile_st_hmr_pc_kernel(tc, h_new, c_new, g_s, c_g_s, Wg_s, Zg_s_bytes, Zg_s_s
                 a, b = k * c0 // n, (k + 1) * c0 // n
                 v_il(wil_tile(g)[:, a:b, :], wraw[g][:, :, a:b])
 
+        def zil_tile(g):
+            if g not in zil:
+                zil[g] = zpool.tile([P, width[g], 4], BF16, name="zil", tag="zil", align_bytes=64)
+            return zil[g]
+
+        def il_z_gpsimd(g):
+            a = width[g] - SHARE_GZ[g]
+            if a < width[g]:
+                nc.gpsimd.tensor_scalar(out=zil_tile(g)[:, a:width[g], :].rearrange("p (g i) j -> p g j i", i=4),
+                                        in0=zwide_of(g, a, width[g]).rearrange("p j (g i) -> p g j i", i=4),
+                                        scalar1=1.0, scalar2=0.0, op0=ALU.mult, op1=ALU.add)
+
         def il_z(g):
-            zil[g] = work.tile([P, width[g], 4], BF16, name="zil", tag="zil", align_bytes=64)
-            v_il(zil[g][:], zwide[g][:])
+            a = width[g] - SHARE_GZ[g]
+            v_il(zil_tile(g)[:, 0:a, :], zwide_of(g, 0, a))
 
         def quant(src, store, g, nm, a=0, b=None):
             if a == 0:
@@ -263,6 +310,9 @@ def tile_st_hmr_pc_kernel(tc, h_new, c_new, g_s, c_g_s, Wg_s, Zg_s_bytes, Zg_s_s
             for k in range(min(limit, len(pend))):
                 u, ft = pend.pop(0)
                 sig(u, ft)
+                if u == 7 and ft == FT - 1:
+                    for f2 in range(RG1_NOW):
+                        reduce_gate(1, f2)
                 if u == UNITS - LATE - 1 and ft == FT - 1:
                     for f2 in range(RG2_SPLIT):
                         reduce_gate(2, f2)
@@ -386,13 +436,13 @@ def tile_st_hmr_pc_kernel(tc, h_new, c_new, g_s, c_g_s, Wg_s, Zg_s_bytes, Zg_s_s
                 turn_h()
             if s == st[7] + TANH_AFTER and not TANH_LAST:
                 tanh_eighth()
-            if SIG_FIRST:
+            if SIG_FIRST or s >= SIG_FIRST_FROM:
                 sigs(SIG_LIMIT)
-            if s + LEAD < NG and s + LEAD not in zwide:
+            if s + LEAD < NG:
                 widen(s + LEAD)
             if s + LEADW < NG:
                 il_w_scalar(s + LEADW)
-            if not SIG_FIRST:
+            if not (SIG_FIRST or s >= SIG_FIRST_FROM):
                 sigs(SIG_LIMIT)
             if s == st[7] + TANH_AFTER and TANH_LAST:
                 tanh_eighth()
@@ -400,11 +450,13 @@ def tile_st_hmr_pc_kernel(tc, h_new, c_new, g_s, c_g_s, Wg_s, Zg_s_bytes, Zg_s_s
                 quant(wil, wq, s, "w")
             if s < NG:
                 il_z(s)
+            if s == CELL_BEHIND_ILZ:
+                new_cell()
             if s < NG and s not in Q_PIECES and s not in QW_FIRST:
                 quant(wil, wq, s, "w")
             if FC_EARLY:
                 for ft in range(FT):
-                    if st[3] + FC_AFTER + ft // FC_PER_STAGE == s:
+                    if FC_SLOTS[ft] == (s, "A"):
                         f_times_c(ft)
                 if s + 2 < NG:
                     il_w_gpsimd(s + 2)
@@ -415,6 +467,14 @@ def tile_st_hmr_pc_kernel(tc, h_new, c_new, g_s, c_g_s, Wg_s, Zg_s_bytes, Zg_s_s
             if s < NG and s not in Q_PIECES:
                 quant(zil, zq, s, "z")
                 waiting.append(s)
+            if FC_EARLY:
+                for ft in range(FT):
+                    if FC_SLOTS[ft] == (s, "B"):
+                        f_times_c(ft)
+                if CELL_SLOT == s:
+                    new_cell()
+                if s + 1 < NG:
+                    il_z_gpsimd(s + 1)
             if s in Q_PIECES:
                 n = Q_PIECES[s]
                 w = width[s] // n
@@ -439,10 +499,10 @@ def tile_st_hmr_pc_kernel(tc, h_new, c_new, g_s, c_g_s, Wg_s, Zg_s_bytes, Zg_s_s
             for ft in range(FT):
                 if st[3] + FC_AFTER + ft // FC_PER_STAGE == s and not FC_EARLY:
                     f_times_c(ft)
-            for ft in range(FT):
-                if st[7] + 1 + ft // RG1_PER_STAGE == s:
+            for ft in range(RG1_NOW, FT):
+                if st[7] + 1 + (ft - RG1_NOW) // RG1_PER_STAGE == s:
                     reduce_gate(1, ft)
-            if s == st[7] + CELL_AFTER:
+            if s == st[7] + CELL_AFTER and CELL_SLOT < 0 and CELL_BEHIND_ILZ < 0:
                 new_cell()
             for ft in rg2:
                 reduce_gate(2, ft)

@@ -21,9 +21,9 @@ UNITS = GH * T
 COLS = NB * B
 
 GROUPS = [[(u, 0, H)] for u in range(UNITS)]
-SHARE_W = [0, 0, 0, 0, 0, 0, 160, 96, 64, 64, 64, 128]
-LOADS = ["zscale","z0","w0","z0.0","w0.0","z0.1","w0.1","z0.2","w0.2","z0.3","w0.3","z1","w1","z2","h","gs","bias","w2","z3","w3","c","z4","w4","z5","w5"]
-LATER = ["z6", "w6", "z7", "w7", "z8", "w8", "z9", "w9", "z10", "w10", "cgs", "z11", "w11"]
+SHARE_W = [0, 0, 0, 0, 0, 0, 160, 96, 64, 128, 128, 192]
+LOADS = ["zscale","z0","w0","z0.0","w0.0","z0.1","w0.1","z0.2","w0.2","z0.3","w0.3","z1","w1","z2","h","gs","bias","w2","z3","w3","z4","z5","c","w4","w5"]
+LATER = ["z6","z7","w6","w7","z8","z9","w8","w9","z10","z11","cgs","w10","w11"]
 LOADS_PER_STAGE = 2
 RAWBUFS = 6
 WIDEBUFS = 4
@@ -66,7 +66,7 @@ ZILBUFS = 4
 SHARE_GZ = [0] * 12
 FC_SLOTS = [(5, "A"), (6, "A"), (7, "A"), (8, "A")]
 CELL_SLOT = -1
-ZGROUPS = [[g] for g in range(12)]
+ZGROUPS = [[0], [1], [2], [3], [4, 5], [6, 7], [8, 9], [10, 11]]
 SIG_FIRST_FROM = 99
 RG1_NOW = 0
 CELL_BEHIND_ILZ = -1

@@ -62,16 +62,20 @@ REPL_DMA = False
 QW_FIRST = []
 IL_FORM = "runs"
 IL_RUN = 4
-ZILBUFS = 4
-SHARE_GZ = [0] * 12
+ZILBUFS = 1
+SHARE_GZ = [0, 0, 0, 0, 0, 0, 0, 0, 0, 0, 0, 152]
 FC_SLOTS = [(5, "A"), (6, "A"), (7, "A"), (8, "A")]
-CELL_SLOT = -1
+CELL_SLOT = 10
 ZGROUPS = [[0], [1], [2], [3], [4, 5], [6, 7], [8, 9], [10, 11]]
 SIG_FIRST_FROM = 99
 RG1_NOW = 0
 CELL_BEHIND_ILZ = -1
-WIDEN_ON_V = []
+WIDEN_ON_V = {}
 PIN_ALL = False
+PIN_SCALAR = True
+G_EARLY = False
+QZ_LATE = []
+H_ON_V = []
 
 NG = len(GROUPS)
 FLOPS = 2 * (B * NB + B) * H * H * GH * T
@@ -93,7 +97,10 @@ def tile_st_hmr_pc_kernel(tc, h_new, c_new, g_s, c_g_s, Wg_s, Zg_s_bytes, Zg_s_s
             ctx.enter_context(tc.manual_schedule())
         else:
             ET = mybir.EngineType
-            ctx.enter_context(tc.manual_schedule(engines={ET.DVE, ET.Activation, ET.Pool, ET.SP}))
+            if PIN_SCALAR:
+                ctx.enter_context(tc.manual_schedule(engines={ET.DVE, ET.Activation, ET.Pool, ET.SP}))
+            else:
+                ctx.enter_context(tc.manual_schedule(engines={ET.DVE, ET.Pool, ET.SP}))
 
         warm = const.tile([P, 1], F32, name="warm")
         nc.vector.memset(warm[:], 0.0)
@@ -195,7 +202,7 @@ def tile_st_hmr_pc_kernel(tc, h_new, c_new, g_s, c_g_s, Wg_s, Zg_s_bytes, Zg_s_s
                 return
             zwide[k] = wide.tile([P, 4, zwidth[k]], BF16, name="zwide", tag="zwide")
             for j in range(4):
-                if g in WIDEN_ON_V:
+                if g in WIDEN_ON_V and j in WIDEN_ON_V[g]:
                     nc.vector.tensor_scalar(out=zwide[k][:, j, :], in0=zbytes[k][:, j, :].bitcast(FP8), scalar1=zscale[:, j:j + 1],
                                             scalar2=None, op0=ALU.mult)
                     continue
@@ -360,7 +367,10 @@ def tile_st_hmr_pc_kernel(tc, h_new, c_new, g_s, c_g_s, Wg_s, Zg_s_bytes, Zg_s_s
                     hT = aux.tile([P, HT_N, 2, P], F32, name="hT", tag="aux")
                 for u in range(2):
                     nc.tensor.transpose(hT[:, n % HT_N, u, :], hw[:, n, u::2], ident_f[:])
-                nc.scalar.copy(out=hin_w[:, :, n, :, :], in_=hT[:, n % HT_N].rearrange("p u (b t) -> p t b u", t=T))
+                if n in H_ON_V:
+                    nc.vector.tensor_copy(out=hin_w[:, :, n, :, :], in_=hT[:, n % HT_N].rearrange("p u (b t) -> p t b u", t=T))
+                else:
+                    nc.scalar.copy(out=hin_w[:, :, n, :, :], in_=hT[:, n % HT_N].rearrange("p u (b t) -> p t b u", t=T))
             gw = gs_sb[:].bitcast(F32)
             gT = aux.tile([P, 2, P], F32, name="gT", tag="aux")
             for u in range(2):
@@ -448,6 +458,8 @@ def tile_st_hmr_pc_kernel(tc, h_new, c_new, g_s, c_g_s, Wg_s, Zg_s_bytes, Zg_s_s
                 tanh_eighth()
             if s in QW_FIRST:
                 quant(wil, wq, s, "w")
+                if FC_EARLY and s + 2 < NG and G_EARLY:
+                    il_w_gpsimd(s + 2)
             if s < NG:
                 il_z(s)
             if s == CELL_BEHIND_ILZ:
@@ -458,9 +470,9 @@ def tile_st_hmr_pc_kernel(tc, h_new, c_new, g_s, c_g_s, Wg_s, Zg_s_bytes, Zg_s_s
                 for ft in range(FT):
                     if FC_SLOTS[ft] == (s, "A"):
                         f_times_c(ft)
-                if s + 2 < NG:
+                if s + 2 < NG and not (G_EARLY and s in QW_FIRST):
                     il_w_gpsimd(s + 2)
-            if s + LEADW < NG and not QZ_EARLY:
+            if s + LEADW < NG and (not QZ_EARLY or s in QZ_LATE):
                 il_w(s + LEADW)
             if s == EARLY_OUT:
                 early_out()
@@ -485,7 +497,7 @@ def tile_st_hmr_pc_kernel(tc, h_new, c_new, g_s, c_g_s, Wg_s, Zg_s_bytes, Zg_s_s
                     if k in WEAVE_AFTER and rg2:
                         reduce_gate(2, rg2[0])
                         rg2.remove(rg2[0])
-            if s + LEADW < NG and QZ_EARLY:
+            if s + LEADW < NG and QZ_EARLY and s not in QZ_LATE:
                 il_w(s + LEADW)
             if s == QUANT_H:
                 quant_h()

@@ -19,65 +19,32 @@ B, T, NB, H, GH = 32, 4, 8, 512, 3
 FT = H // P
 UNITS = GH * T
 COLS = NB * B
+LAST = UNITS - 1
 
-GROUPS = [[(u, 0, H)] for u in range(UNITS)]
-SHARE_W = [0, 0, 0, 0, 0, 0, 160, 96, 64, 128, 128, 192]
-LOADS = ["zscale","z0","w0","z0.0","w0.0","z0.1","w0.1","z0.2","w0.2","z0.3","w0.3","z1","w1","z2","h","gs","bias","w2","z3","w3","z4","z5","c","w4","w5"]
-LATER = ["z6","z7","w6","w7","z8","z9","w8","w9","z10","z11","cgs","w10","w11"]
-LOADS_PER_STAGE = 2
-RAWBUFS = 6
-WIDEBUFS = 4
-WORKBUFS = 4
-CODEBUFS = 4
-LEAD = 2
-LEADW = 1
-LATE = 1
-TURN_H = 0
-QUANT_H = 1
-TURN_C = 2
-FC_PER_STAGE = 1
-RG1_PER_STAGE = 2
-CELL_AFTER = 3
-TANH_AFTER = 4
-RG2_SPLIT = 3
-EARLY_OUT = 104
-SIG_FIRST = False
-SIG_LIMIT = 8
-FC_AFTER = 2
-FLUSH_AT = [10]
-HT_N = 1
-QZ_EARLY = True
-Z_BY_PLANE = [0]
-W_CHUNKS = {0: 4}
-Q_PIECES = {11: 4}
-END_STEP = 4
-HEAD_EXTRA = 1
-AFFINE_ON_S = True
-TANH_LAST = False
-WEAVE_AFTER = [3]
-WILBUFS = 2
-SHARE_G = [0, 0, 0, 0, 0, 0, 0, 152, 152, 152, 152, 0]
-FC_EARLY = True
-REPL_DMA = False
-QW_FIRST = []
-IL_FORM = "runs"
-IL_RUN = 4
-ZILBUFS = 1
-SHARE_GZ = [0, 0, 0, 0, 0, 0, 0, 0, 0, 0, 0, 152]
-FC_SLOTS = [(5, "A"), (6, "A"), (7, "A"), (8, "A")]
-CELL_SLOT = 10
+PIN_PE = True
+LOADS = ["zscale", "z0.0", "w0.0", "z0.1", "w0.1", "z0.2", "w0.2", "z0.3", "w0.3", "z1", "w1", "z2", "h", "gs", "bias", "w2", "z3", "w3", "z4", "z5", "c", "w4", "w5"]
+LATER = ["z6", "z7", "w6", "w7", "z8", "z9", "w8", "w9", "z10", "z11", "cgs", "w10", "w11"]
 ZGROUPS = [[0], [1], [2], [3], [4, 5], [6, 7], [8, 9], [10, 11]]
-SIG_FIRST_FROM = 99
-RG1_NOW = 0
-CELL_BEHIND_ILZ = -1
-WIDEN_ON_V = {}
-PIN_ALL = False
-PIN_SCALAR = True
-G_EARLY = False
-QZ_LATE = []
-H_ON_V = []
-
-NG = len(GROUPS)
+W_PE = [0, 0, 0, 0, 0, 0, 0, 0, 0, 0, 0, 0]
+W_S = [0, 0, 0, 0, 0, 0, 160, 96, 64, 128, 128, 192]
+W_G = [0, 0, 0, 0, 0, 0, 0, 152, 152, 152, 152, 0]
+Z_G = [0, 0, 0, 0, 0, 0, 0, 0, 0, 0, 0, 152]
+Z_ON_V = {}
+IL_FIRST = []
+FC_AT = [5, 6, 7, 8]
+CT_AT = [2, 2, 2, 6]
+RG1_AT = [9, 9, 10, 10]
+CELL_AT = 10
+QW0_FIRST = False
+G_FIRST = True
+CELL_PARTS = 2
+MX_BANKS = 4
+CT_BANKS = 3
+LATE_STEP = 4
+EARLY_SUMS = 2
+EARLY_FIRST = True
+AFFINE_ON_S = True
+TAIL_SPLIT = False
 FLOPS = 2 * (B * NB + B) * H * H * GH * T
 
 
@@ -85,22 +52,18 @@ def tile_st_hmr_pc_kernel(tc, h_new, c_new, g_s, c_g_s, Wg_s, Zg_s_bytes, Zg_s_s
     nc = tc.nc
     with ExitStack() as ctx:
         const = ctx.enter_context(tc.tile_pool(name="const", bufs=1))
-        raw = ctx.enter_context(tc.tile_pool(name="raw", bufs=RAWBUFS))
-        wide = ctx.enter_context(tc.tile_pool(name="wide", bufs=WIDEBUFS))
-        work = ctx.enter_context(tc.tile_pool(name="work", bufs=WORKBUFS))
-        wpool = ctx.enter_context(tc.tile_pool(name="wpool", bufs=WILBUFS))
-        zpool = ctx.enter_context(tc.tile_pool(name="zpool", bufs=ZILBUFS))
-        codes = ctx.enter_context(tc.tile_pool(name="codes", bufs=CODEBUFS))
-        mxps = ctx.enter_context(tc.psum_pool(name="mxps", bufs=4))
-        aux = ctx.enter_context(tc.psum_pool(name="aux", bufs=4))
-        if PIN_ALL:
+        raw = ctx.enter_context(tc.tile_pool(name="raw", bufs=6))
+        wide = ctx.enter_context(tc.tile_pool(name="wide", bufs=4))
+        wpool = ctx.enter_context(tc.tile_pool(name="wpool", bufs=2))
+        zpool = ctx.enter_context(tc.tile_pool(name="zpool", bufs=1))
+        codes = ctx.enter_context(tc.tile_pool(name="codes", bufs=4))
+        mxps = ctx.enter_context(tc.psum_pool(name="mxps", bufs=MX_BANKS))
+        aux = ctx.enter_context(tc.psum_pool(name="aux", bufs=1))
+        if PIN_PE:
             ctx.enter_context(tc.manual_schedule())
         else:
             ET = mybir.EngineType
-            if PIN_SCALAR:
-                ctx.enter_context(tc.manual_schedule(engines={ET.DVE, ET.Activation, ET.Pool, ET.SP}))
-            else:
-                ctx.enter_context(tc.manual_schedule(engines={ET.DVE, ET.Pool, ET.SP}))
+            ctx.enter_context(tc.manual_schedule(engines={ET.DVE, ET.Activation, ET.Pool, ET.SP}))
 
         warm = const.tile([P, 1], F32, name="warm")
         nc.vector.memset(warm[:], 0.0)
@@ -138,7 +101,7 @@ def tile_st_hmr_pc_kernel(tc, h_new, c_new, g_s, c_g_s, Wg_s, Zg_s_bytes, Zg_s_s
         for ft in range(FT):
             gate_a[ft] = const.tile([P, NB, T, B], F32, name="gate_a%d" % ft)
             gate_b[ft] = const.tile([P, NB, T, B], F32, name="gate_b%d" % ft)
-        last = const.tile([P, FT, NB, LATE, B], F32, name="last")
+        last = const.tile([P, FT, NB, B], F32, name="last")
 
         zbytes = {}
         wraw = {}
@@ -150,190 +113,23 @@ def tile_st_hmr_pc_kernel(tc, h_new, c_new, g_s, c_g_s, Wg_s, Zg_s_bytes, Zg_s_s
         mxp = {}
         cT = {}
         acc = {}
-        width = [sum(c1 - c0 for (u, c0, c1) in grp) for grp in GROUPS]
-        st = {}
-        for g in range(NG):
-            for (u, c0, c1) in GROUPS[g]:
-                st[u] = g
-
+        pe_il = {}
+        small = {}
         zg_of = {}
         for k in range(len(ZGROUPS)):
-            o = 0
-            for g in ZGROUPS[k]:
-                zg_of[g] = (k, o)
-                o += width[g]
-        zwidth = [sum(width[g] for g in grp) for grp in ZGROUPS]
+            for i in range(len(ZGROUPS[k])):
+                zg_of[ZGROUPS[k][i]] = (k, i * H)
 
-        def load_z(g):
-            k, o = zg_of[g]
-            if o == 0:
-                zbytes[k] = raw.tile([P, 4, zwidth[k]], U8, name="zbytes", tag="zbytes")
-            for (u, c0, c1) in GROUPS[g]:
-                src = Zg_s_bytes[u // T, u % T].rearrange("(p j) n -> p j n", j=4)
-                if g in Z_BY_PLANE:
-                    continue
-                nc.sync.dma_start(out=zbytes[k][:, :, o:o + c1 - c0], in_=src[:, :, c0:c1])
-                o += c1 - c0
+        def z_src(u):
+            return Zg_s_bytes[u // T, u % T].rearrange("(p j) n -> p j n", j=4)
 
-        def load_z_plane(g, j):
-            (u, c0, c1) = GROUPS[g][0]
-            src = Zg_s_bytes[u // T, u % T].rearrange("(p j) n -> p j n", j=4)
-            nc.sync.dma_start(out=zbytes[zg_of[g][0]][:, j, :], in_=src[:, j, c0:c1])
-
-        def load_w(g):
-            wraw[g] = raw.tile([P, 4, width[g]], BF16, name="wraw", tag="wraw")
-            o = 0
-            for (u, c0, c1) in GROUPS[g]:
-                if g in W_CHUNKS:
-                    continue
-                nc.sync.dma_start(out=wraw[g][:, :, o:o + c1 - c0],
-                                  in_=Wg_s[u // T, u % T].rearrange("(p j) n -> p j n", j=4)[:, :, c0:c1])
-                o += c1 - c0
-
-        def load_w_chunk(g, k):
-            (u, c0, c1) = GROUPS[g][0]
-            w = (c1 - c0) // W_CHUNKS[g]
-            nc.sync.dma_start(out=wraw[g][:, :, k * w:(k + 1) * w],
-                              in_=Wg_s[u // T, u % T].rearrange("(p j) n -> p j n", j=4)[:, :, c0 + k * w:c0 + (k + 1) * w])
-
-        def widen(g):
-            k, o = zg_of[g]
-            if k in zwide:
-                return
-            zwide[k] = wide.tile([P, 4, zwidth[k]], BF16, name="zwide", tag="zwide")
-            for j in range(4):
-                if g in WIDEN_ON_V and j in WIDEN_ON_V[g]:
-                    nc.vector.tensor_scalar(out=zwide[k][:, j, :], in0=zbytes[k][:, j, :].bitcast(FP8), scalar1=zscale[:, j:j + 1],
-                                            scalar2=None, op0=ALU.mult)
-                    continue
-                nc.scalar.activation(out=zwide[k][:, j, :], in_=zbytes[k][:, j, :].bitcast(FP8), func=ACT.Copy,
-                                     scale=zscale[:, j:j + 1])
-
-        def zwide_of(g, a, b):
-            k, o = zg_of[g]
-            return zwide[k][:, :, o + a:o + b]
-
-        def v_il(dst, src):
-            if IL_FORM == "halves":
-                nc.vector.tensor_copy(out=dst.rearrange("p c (h j) -> p h c j", h=2), in_=src.rearrange("p (h j) c -> p h c j", h=2))
-            else:
-                nc.vector.tensor_copy(out=dst.rearrange("p (g i) j -> p g j i", i=IL_RUN),
-                                      in_=src.rearrange("p j (g i) -> p g j i", i=IL_RUN))
-
-        def wil_tile(g):
-            if g not in wil:
-                wil[g] = wpool.tile([P, width[g], 4], BF16, name="wil", tag="wil", align_bytes=64)
-            return wil[g]
-
-        def il_w_scalar(g):
-            c0 = width[g] - SHARE_W[g]
-            if c0 < width[g]:
-                nc.scalar.copy(out=wil_tile(g)[:, c0:width[g], :].rearrange("p (g i) j -> p g j i", i=4),
-                               in_=wraw[g][:, :, c0:width[g]].rearrange("p j (g i) -> p g j i", i=4))
-
-        def il_w_gpsimd(g):
-            b = width[g] - SHARE_W[g]
-            a = b - SHARE_G[g]
-            if a < b:
-                nc.gpsimd.tensor_scalar(out=wil_tile(g)[:, a:b, :].rearrange("p (g i) j -> p g j i", i=4),
-                                        in0=wraw[g][:, :, a:b].rearrange("p j (g i) -> p g j i", i=4),
-                                        scalar1=1.0, scalar2=0.0, op0=ALU.mult, op1=ALU.add)
-
-        def il_w(g):
-            c0 = width[g] - SHARE_W[g] - SHARE_G[g]
-            n = W_CHUNKS.get(g, 1)
-            for k in range(n):
-                a, b = k * c0 // n, (k + 1) * c0 // n
-                v_il(wil_tile(g)[:, a:b, :], wraw[g][:, :, a:b])
-
-        def zil_tile(g):
-            if g not in zil:
-                zil[g] = zpool.tile([P, width[g], 4], BF16, name="zil", tag="zil", align_bytes=64)
-            return zil[g]
-
-        def il_z_gpsimd(g):
-            a = width[g] - SHARE_GZ[g]
-            if a < width[g]:
-                nc.gpsimd.tensor_scalar(out=zil_tile(g)[:, a:width[g], :].rearrange("p (g i) j -> p g j i", i=4),
-                                        in0=zwide_of(g, a, width[g]).rearrange("p j (g i) -> p g j i", i=4),
-                                        scalar1=1.0, scalar2=0.0, op0=ALU.mult, op1=ALU.add)
-
-        def il_z(g):
-            a = width[g] - SHARE_GZ[g]
-            v_il(zil_tile(g)[:, 0:a, :], zwide_of(g, 0, a))
-
-        def quant(src, store, g, nm, a=0, b=None):
-            if a == 0:
-                q = codes.tile([P, width[g]], U32, name=nm + "q", tag=nm + "q", align_bytes=64)
-                s = codes.tile([P, width[g]], U8, name=nm + "s", tag=nm + "s", align_bytes=64)
-                store[g] = (q, s)
-            q, s = store[g]
-            if b is None:
-                b = width[g]
-            nc.vector.quantize_mx(out=q[:, a:b].bitcast(FP8X4), scales=s[:, a:b],
-                                  in_=src[g][:, a:b, :].rearrange("p c j -> p (c j)"))
-
-        pend = []
-
-        def mm(g, only=None):
-            o = 0
-            for (u, c0, c1) in GROUPS[g]:
-                t = u % T
-                cols = slice(t * COLS, (t + 1) * COLS)
-                for ft in range(c0 // P, c1 // P):
-                    if only is not None and ft not in only:
-                        continue
-                    if g in Q_PIECES:
-                        mxp[(u, ft)] = mxps.tile([P, COLS], F32, name="mxp", tag="mxp")
-                        ps = mxp[(u, ft)][:]
-                    else:
-                        if ft % 2 == 0:
-                            mxp[(u, ft // 2)] = mxps.tile([P, 2, COLS], F32, name="mxp", tag="mxp")
-                        ps = mxp[(u, ft // 2)][:, ft % 2, :]
-                    fs = slice(o + ft * P - c0, o + (ft + 1) * P - c0)
-                    nc.tensor.matmul_mx(out=ps, lhsT=wq[g][0][:, fs].bitcast(FP8X4), lhsT_scale=wq[g][1][:, fs],
-                                        rhs=hq[:, cols].bitcast(FP8X4), rhs_scale=hs[:, cols], start=True, stop=False)
-                    nc.tensor.matmul_mx(out=ps, lhsT=zq[g][0][:, fs].bitcast(FP8X4), lhsT_scale=zq[g][1][:, fs],
-                                        rhs=gq[:, cols].bitcast(FP8X4), rhs_scale=gsc[:, cols], start=False, stop=True)
-                    pend.append((u, ft))
-                o += c1 - c0
-
-        def sig(u, ft):
-            g, t = u // T, u % T
-            if u >= UNITS - LATE:
-                dst = last[:, ft, :, u - (UNITS - LATE), :]
-            elif g == 1:
-                dst = gate_b[ft][:, :, t, :]
-            else:
-                dst = gate_a[ft][:, :, t, :]
-            col = u * FT + ft
-            src = mxp[(u, ft)][:] if st[u] in Q_PIECES else mxp[(u, ft // 2)][:, ft % 2, :]
-            nc.scalar.activation(out=dst, in_=src.rearrange("p (n b) -> p n b", b=B),
-                                 func=ACT.Sigmoid, bias=bias_sb[:, col:col + 1], scale=1.0)
-
-        rg2 = []
-
-        def sigs(limit):
-            for k in range(min(limit, len(pend))):
-                u, ft = pend.pop(0)
-                sig(u, ft)
-                if u == 7 and ft == FT - 1:
-                    for f2 in range(RG1_NOW):
-                        reduce_gate(1, f2)
-                if u == UNITS - LATE - 1 and ft == FT - 1:
-                    for f2 in range(RG2_SPLIT):
-                        reduce_gate(2, f2)
-                    rg2.extend(range(RG2_SPLIT, FT))
-
-        def reduce_gate(g, ft):
-            if ft == 0:
-                acc[g] = aux.tile([P, H], F32, name="acc", tag="aux")
-            src = gate_b[ft] if g == 1 else gate_a[ft]
-            for n in range(NB):
-                nc.tensor.matmul(out=acc[g][:, ft * P:(ft + 1) * P], lhsT=src[:, n].rearrange("p t b -> p (t b)"),
-                                 rhs=ident_f[:], is_transpose=True, start=(n == 0), stop=(n == NB - 1))
+        def w_src(u):
+            return Wg_s[u // T, u % T].rearrange("(p j) n -> p j n", j=4)
 
         def load_named(what):
+            part = None
+            if "." in what:
+                what, part = what.split(".")
             if what == "zscale":
                 nc.sync.dma_start(out=zscale[:], in_=Zg_s_scale[0, 0].rearrange("(p j) c -> p (j c)", j=4))
             elif what == "h":
@@ -341,206 +137,343 @@ def tile_st_hmr_pc_kernel(tc, h_new, c_new, g_s, c_g_s, Wg_s, Zg_s_bytes, Zg_s_s
             elif what == "gs":
                 nc.sync.dma_start(out=gs_sb[:], in_=g_s.rearrange("b t h -> (b t) h"))
             elif what == "bias":
-                nc.sync.dma_start(out=bias_raw[0:UNITS * FT, :], in_=bg_s.rearrange("g t o (c f) -> (g t o c) f", f=P))
+                rows = bg_s.rearrange("g t o (c f) -> (g t o c) f", f=P)
+                nc.sync.dma_start(out=bias_raw[0:32, :], in_=rows[0:32])
+                nc.sync.dma_start(out=bias_raw[32:48, :], in_=rows[32:48])
             elif what == "c":
                 nc.sync.dma_start(out=c_sb[:], in_=c_new.rearrange("b t n h -> (b t) n h"))
             elif what == "cgs":
                 for t in range(T):
                     nc.sync.dma_start(out=cgs[t * B:(t + 1) * B, :], in_=c_g_s[:, t, :])
-            elif what[0] == "w" and "." in what:
-                load_w_chunk(int(what[1:].split(".")[0]), int(what.split(".")[1]))
-            elif what[0] == "z" and "." in what:
-                load_z_plane(int(what[1:].split(".")[0]), int(what.split(".")[1]))
             elif what[0] == "w":
-                load_w(int(what[1:]))
+                u = int(what[1:])
+                if u not in wraw:
+                    wraw[u] = raw.tile([P, 4, H], BF16, name="wraw", tag="wraw")
+                cs = slice(0, H) if part is None else slice(int(part) * P, (int(part) + 1) * P)
+                nc.sync.dma_start(out=wraw[u][:, :, cs], in_=w_src(u)[:, :, cs])
             else:
-                load_z(int(what[1:]))
+                u = int(what[1:])
+                k, o = zg_of[u]
+                if k not in zbytes:
+                    zbytes[k] = raw.tile([P, 4, H * len(ZGROUPS[k])], U8, name="zbytes", tag="zbytes")
+                if part is None:
+                    nc.sync.dma_start(out=zbytes[k][:, :, o:o + H], in_=z_src(u))
+                else:
+                    nc.sync.dma_start(out=zbytes[k][:, int(part), o:o + H], in_=z_src(u)[:, int(part)])
+
+        def widen(u):
+            k, o = zg_of[u]
+            if k in zwide:
+                return
+            zwide[k] = wide.tile([P, 4, H * len(ZGROUPS[k])], BF16, name="zwide", tag="zwide")
+            for j in range(4):
+                if k in Z_ON_V and j in Z_ON_V[k]:
+                    continue
+                nc.scalar.activation(out=zwide[k][:, j, :], in_=zbytes[k][:, j, :].bitcast(FP8), func=ACT.Copy, scale=zscale[:, j:j + 1])
+
+        def widen_v(u):
+            k, o = zg_of.get(u, (0, 1))
+            if o == 0 and k in Z_ON_V:
+                for j in Z_ON_V[k]:
+                    nc.vector.tensor_scalar(out=zwide[k][:, j, :], in0=zbytes[k][:, j, :].bitcast(FP8), scalar1=zscale[:, j:j + 1],
+                                            scalar2=None, op0=ALU.mult)
+
+        def runs(ap):
+            return ap.rearrange("p (g i) j -> p g j i", i=4)
+
+        def rows(ap):
+            return ap.rearrange("p j (g i) -> p g j i", i=4)
+
+        def wil_of(u):
+            if u not in wil:
+                wil[u] = wpool.tile([P, H, 4], BF16, name="wil", tag="wil", align_bytes=64)
+            return wil[u]
+
+        def zil_of(u):
+            if u not in zil:
+                zil[u] = zpool.tile([P, H, 4], BF16, name="zil", tag="zil", align_bytes=64)
+            return zil[u]
+
+        def zw(u, a, b):
+            k, o = zg_of[u]
+            return zwide[k][:, :, o + a:o + b]
+
+        def il_w_pe(u):
+            n = W_PE[u]
+            if n:
+                pe_il[u] = aux.tile([P, n, 4], BF16, name="pe_il", tag="il")
+                for a in range(0, n, P):
+                    nc.tensor.matmul(out=pe_il[u][:, a:a + P, :], lhsT=ident_b[:],
+                                     rhs=wraw[u][:, :, H - n + a:H - n + a + P].rearrange("p j c -> p c j"), start=True, stop=True)
+
+        def il_w_s(u):
+            e = H - W_PE[u]
+            if W_PE[u]:
+                nc.scalar.copy(out=wil_of(u)[:, e:H, :], in_=pe_il[u][:])
+            if W_S[u]:
+                a = e - W_S[u]
+                nc.scalar.copy(out=runs(wil_of(u)[:, a:e, :]), in_=rows(wraw[u][:, :, a:e]))
+
+        def il_w_g(u):
+            e = H - W_PE[u] - W_S[u]
+            if W_G[u]:
+                a = e - W_G[u]
+                nc.gpsimd.tensor_scalar(out=runs(wil_of(u)[:, a:e, :]), in0=rows(wraw[u][:, :, a:e]), scalar1=1.0, scalar2=0.0,
+                                        op0=ALU.mult, op1=ALU.add)
+
+        def il_w(u, a=0, b=H):
+            b = min(b, H - W_PE[u] - W_S[u] - W_G[u])
+            if a < b:
+                nc.vector.tensor_copy(out=runs(wil_of(u)[:, a:b, :]), in_=rows(wraw[u][:, :, a:b]))
+
+        def il_z_g(u):
+            if Z_G[u]:
+                a = H - Z_G[u]
+                nc.gpsimd.tensor_scalar(out=runs(zil_of(u)[:, a:H, :]), in0=rows(zw(u, a, H)), scalar1=1.0, scalar2=0.0,
+                                        op0=ALU.mult, op1=ALU.add)
+
+        def il_z(u, a=0, b=H):
+            b = min(b, H - Z_G[u])
+            if a < b:
+                nc.vector.tensor_copy(out=runs(zil_of(u)[:, a:b, :]), in_=rows(zw(u, a, b)))
+
+        def quant(src, store, u, nm, a=0, b=H):
+            if u not in store:
+                store[u] = (codes.tile([P, H], U32, name=nm + "q", tag=nm + "q", align_bytes=64),
+                            codes.tile([P, H], U8, name=nm + "s", tag=nm + "s", align_bytes=64))
+            q, s = store[u]
+            nc.vector.quantize_mx(out=q[:, a:b].bitcast(FP8X4), scales=s[:, a:b], in_=src[u][:, a:b, :].rearrange("p c j -> p (c j)"))
+
+        pend = []
+
+        def mm(u, fts):
+            t = u % T
+            cols = slice(t * COLS, (t + 1) * COLS)
+            for ft in fts:
+                if u == LAST:
+                    mxp[(u, ft)] = mxps.tile([P, COLS], F32, name="mxp", tag="mxp")
+                    ps = mxp[(u, ft)][:]
+                else:
+                    if ft % 2 == 0:
+                        mxp[(u, ft // 2)] = mxps.tile([P, 2, COLS], F32, name="mxp", tag="mxp")
+                    ps = mxp[(u, ft // 2)][:, ft % 2, :]
+                fs = slice(ft * P, (ft + 1) * P)
+                nc.tensor.matmul_mx(out=ps, lhsT=wq[u][0][:, fs].bitcast(FP8X4), lhsT_scale=wq[u][1][:, fs],
+                                    rhs=hq[:, cols].bitcast(FP8X4), rhs_scale=hs[:, cols], start=True, stop=False)
+                nc.tensor.matmul_mx(out=ps, lhsT=zq[u][0][:, fs].bitcast(FP8X4), lhsT_scale=zq[u][1][:, fs],
+                                    rhs=gq[:, cols].bitcast(FP8X4), rhs_scale=gsc[:, cols], start=False, stop=True)
+                pend.append((u, ft))
+
+        def sigs(n):
+            for k in range(min(n, len(pend))):
+                u, ft = pend.pop(0)
+                g, t = u // T, u % T
+                if u == LAST:
+                    dst, ps = last[:, ft], mxp[(u, ft)][:]
+                else:
+                    dst, ps = (gate_b if g == 1 else gate_a)[ft][:, :, t, :], mxp[(u, ft // 2)][:, ft % 2, :]
+                nc.scalar.activation(out=dst, in_=ps.rearrange("p (n b) -> p n b", b=B), func=ACT.Sigmoid,
+                                     bias=bias_sb[:, u * FT + ft:u * FT + ft + 1], scale=1.0)
+
+        def sum_bones(g, ft, dst):
+            src = gate_b[ft] if g == 1 else gate_a[ft]
+            for n in range(NB):
+                nc.tensor.matmul(out=dst, lhsT=src[:, n].rearrange("p t b -> p (t b)"), rhs=ident_f[:], is_transpose=True,
+                                 start=(n == 0), stop=(n == NB - 1))
 
         hin_w = hin[:].bitcast(F32).rearrange("p (t n b u) -> p t n b u", t=T, n=NB, b=B, u=2)
-        small = {}
 
         def turn_h():
             hw = h_sb[:].bitcast(F32)
-            hT = None
+            tags = [(mxps, "mxp"), (aux, "c0"), (mxps, "mxp"), (aux, "c1"), (mxps, "mxp"), (aux, "c2"), (mxps, "mxp"), (aux, "c3")]
+            if CT_BANKS < 4:
+                tags[7] = (aux, "il")
+            hTs = []
             for n in range(NB):
-                if n % HT_N == 0:
-                    hT = aux.tile([P, HT_N, 2, P], F32, name="hT", tag="aux")
+                pool, tag = tags[n]
+                hT = pool.tile([P, 2, P], F32, name="hT", tag=tag)
                 for u in range(2):
-                    nc.tensor.transpose(hT[:, n % HT_N, u, :], hw[:, n, u::2], ident_f[:])
-                if n in H_ON_V:
-                    nc.vector.tensor_copy(out=hin_w[:, :, n, :, :], in_=hT[:, n % HT_N].rearrange("p u (b t) -> p t b u", t=T))
-                else:
-                    nc.scalar.copy(out=hin_w[:, :, n, :, :], in_=hT[:, n % HT_N].rearrange("p u (b t) -> p t b u", t=T))
+                    nc.tensor.transpose(hT[:, u, :], hw[:, n, u::2], ident_f[:])
+                hTs.append(hT)
+                nc.scalar.copy(out=hin_w[:, :, n, :, :], in_=hT[:].rearrange("p u (b t) -> p t b u", t=T))
             gw = gs_sb[:].bitcast(F32)
-            gT = aux.tile([P, 2, P], F32, name="gT", tag="aux")
+            gT = mxps.tile([P, 2, P], F32, name="gT", tag="mxp")
             for u in range(2):
                 nc.tensor.transpose(gT[:, u, :], gw[:, u::2], ident_f[:])
-            small["bT"] = aux.tile([P, P], BF16, name="bT", tag="aux")
+            small["bT"] = mxps.tile([P, P], BF16, name="bT", tag="mxp")
             nc.tensor.transpose(small["bT"][:], bias_raw[:], ident_b[:])
             nc.scalar.copy(out=gin0[:].bitcast(F32).rearrange("p (t b u) -> p t b u", t=T, b=B, u=2),
                            in_=gT[:].rearrange("p u (b t) -> p t b u", t=T))
 
         def quant_h():
-            nc.vector.tensor_copy(out=bias_sb[:], in_=small["bT"][:, 0:UNITS * FT])
-            nc.vector.quantize_mx(out=hq[:].bitcast(FP8X4), scales=hs[:], in_=hin[:])
-            nc.vector.quantize_mx(out=gq0[:].bitcast(FP8X4), scales=gs0[:], in_=gin0[:])
-            if REPL_DMA:
-                for n in range(NB):
-                    nc.sync.dma_start(out=gq[:].bitcast(I32).rearrange("p (t n b) -> p t n b", t=T, n=NB, b=B)[:, :, n, :],
-                                      in_=gq0[:].bitcast(I32).rearrange("p (t b) -> p t b", t=T))
-                    nc.sync.dma_start(out=gsc[:].bitcast(I32).rearrange("p (t n w) -> p t n w", t=T, n=NB, w=B // 4)[:, :, n, :],
-                                      in_=gs0[:].bitcast(I32).rearrange("p (t w) -> p t w", t=T))
+            if G_FIRST:
+                nc.vector.quantize_mx(out=gq0[:].bitcast(FP8X4), scales=gs0[:], in_=gin0[:])
+                nc.vector.quantize_mx(out=hq[:].bitcast(FP8X4), scales=hs[:], in_=hin[:])
             else:
-                nc.vector.tensor_copy(
-                    out=gq[:].bitcast(I32).rearrange("p (t n b) -> p t n b", t=T, n=NB, b=B),
-                    in_=gq0[:].bitcast(I32).rearrange("p (t b) -> p t b", t=T).unsqueeze(2).to_broadcast([P, T, NB, B]))
-                nc.vector.tensor_copy(
-                    out=gsc[:].bitcast(I32).rearrange("p (t n w) -> p t n w", t=T, n=NB, w=B // 4),
-                    in_=gs0[:].bitcast(I32).rearrange("p (t w) -> p t w", t=T).unsqueeze(2).to_broadcast([P, T, NB, B // 4]))
+                nc.vector.tensor_copy(out=bias_sb[:], in_=small["bT"][:, 0:UNITS * FT])
+                nc.vector.quantize_mx(out=hq[:].bitcast(FP8X4), scales=hs[:], in_=hin[:])
+                nc.vector.quantize_mx(out=gq0[:].bitcast(FP8X4), scales=gs0[:], in_=gin0[:])
+            nc.vector.tensor_copy(
+                out=gq[:].bitcast(I32).rearrange("p (t n b) -> p t n b", t=T, n=NB, b=B),
+                in_=gq0[:].bitcast(I32).rearrange("p (t b) -> p t b", t=T).unsqueeze(2).to_broadcast([P, T, NB, B]))
+            nc.vector.tensor_copy(
+                out=gsc[:].bitcast(I32).rearrange("p (t n w) -> p t n w", t=T, n=NB, w=B // 4),
+                in_=gs0[:].bitcast(I32).rearrange("p (t w) -> p t w", t=T).unsqueeze(2).to_broadcast([P, T, NB, B // 4]))
+            if G_FIRST:
+                nc.vector.tensor_copy(out=bias_sb[:], in_=small["bT"][:, 0:UNITS * FT])
 
-        def turn_c():
-            for ft in range(FT):
-                cT[ft] = aux.tile([P, NB, P], BF16, name="cT", tag="aux")
-                for n in range(NB):
-                    nc.tensor.transpose(cT[ft][:, n, :], c_sb[:, n, ft * P:(ft + 1) * P], ident_b[:])
+        def turn_c(ft):
+            cT[ft] = aux.tile([P, NB, P], BF16, name="cT", tag="c%d" % (ft if ft < CT_BANKS else 1))
+            for n in range(NB):
+                nc.tensor.transpose(cT[ft][:, n, :], c_sb[:, n, ft * P:(ft + 1) * P], ident_b[:])
+
+        def acc_tile(g):
+            tags = ["c0", "c2"]
+            acc[g] = aux.tile([P, H], F32, name="acc", tag=tags[g])
 
         def f_times_c(ft):
             f = gate_a[ft]
             nc.vector.tensor_tensor(out=f[:], in0=f[:], in1=cT[ft][:].rearrange("p n (b t) -> p n t b", t=T), op=ALU.mult)
-            reduce_gate(0, ft)
 
         def new_cell():
-            nc.vector.scalar_tensor_tensor(out=t1[:], in0=acc[1][:], scalar=0.125, in1=cgs[:], op0=ALU.mult, op1=ALU.mult)
-            nc.vector.scalar_tensor_tensor(out=cnew[:], in0=acc[0][:], scalar=0.125, in1=t1[:], op0=ALU.mult, op1=ALU.add)
+            for c in range(0, H, H // CELL_PARTS):
+                cs = slice(c, c + H // CELL_PARTS)
+                nc.vector.scalar_tensor_tensor(out=t1[:, cs], in0=acc[1][:, cs], scalar=0.125, in1=cgs[:, cs], op0=ALU.mult, op1=ALU.mult)
+            for c in range(0, H, H // CELL_PARTS):
+                cs = slice(c, c + H // CELL_PARTS)
+                nc.vector.scalar_tensor_tensor(out=cnew[:, cs], in0=acc[0][:, cs], scalar=0.125, in1=t1[:, cs], op0=ALU.mult, op1=ALU.add)
             for t in range(T):
                 nc.sync.dma_start(out=out_1[:, t, :], in_=cnew[t * B:(t + 1) * B, :])
 
-        def tanh_eighth():
-            nc.scalar.activation(out=s2[:], in_=cnew[:], func=ACT.Sigmoid, scale=2.0)
-            if AFFINE_ON_S:
-                nc.scalar.activation(out=s2[:], in_=s2[:], func=ACT.Copy, scale=0.25, bias=-0.125)
-
-        R = (T - LATE) * B
-
-        def early_out():
-            if not AFFINE_ON_S:
-                nc.vector.tensor_scalar(out=s2[:], in0=s2[:], scalar1=0.25, scalar2=-0.125, op0=ALU.mult, op1=ALU.add)
-            nc.vector.tensor_tensor(out=gnew[0:R, :], in0=acc[2][0:R, :], in1=s2[0:R, :], op=ALU.mult)
-            for t in range(T - LATE):
-                nc.sync.dma_start(out=out_0[:, t, :], in_=gnew[t * B:(t + 1) * B, :])
+        R = (T - 1) * B
 
         for what in LOADS:
             load_named(what)
         later = list(LATER)
+        for u in range(3):
+            widen(u)
+        for c in range(FT):
+            il_w(0, c * P, (c + 1) * P)
 
-        for g in range(LEAD + HEAD_EXTRA):
-            widen(g)
-        for g in range(LEADW):
-            il_w_scalar(g)
-            il_w(g)
-
-        waiting = []
-        have_h = False
-        for s in range(NG + 1):
-            if s == TURN_H:
+        for s in range(UNITS):
+            if s == 0:
                 turn_h()
-            if s == st[7] + TANH_AFTER and not TANH_LAST:
-                tanh_eighth()
-            if SIG_FIRST or s >= SIG_FIRST_FROM:
-                sigs(SIG_LIMIT)
-            if s + LEAD < NG:
-                widen(s + LEAD)
-            if s + LEADW < NG:
-                il_w_scalar(s + LEADW)
-            if not (SIG_FIRST or s >= SIG_FIRST_FROM):
-                sigs(SIG_LIMIT)
-            if s == st[7] + TANH_AFTER and TANH_LAST:
-                tanh_eighth()
-            if s in QW_FIRST:
+            if s + 2 < UNITS and s not in IL_FIRST:
+                widen(s + 2)
+            if s + 1 < UNITS:
+                il_w_s(s + 1)
+            if s + 2 < UNITS and s in IL_FIRST:
+                widen(s + 2)
+            if s + 2 < UNITS:
+                il_w_pe(s + 2)
+            sigs(8)
+            if s == LAST:
+                break
+            if s == 0 and QW0_FIRST:
                 quant(wil, wq, s, "w")
-                if FC_EARLY and s + 2 < NG and G_EARLY:
-                    il_w_gpsimd(s + 2)
-            if s < NG:
                 il_z(s)
-            if s == CELL_BEHIND_ILZ:
-                new_cell()
-            if s < NG and s not in Q_PIECES and s not in QW_FIRST:
+            else:
+                il_z(s)
                 quant(wil, wq, s, "w")
-            if FC_EARLY:
+            if s in FC_AT:
+                ft = FC_AT.index(s)
+                f_times_c(ft)
+                if ft == 0:
+                    acc_tile(0)
+                sum_bones(0, ft, acc[0][:, ft * P:(ft + 1) * P])
+            if s + 2 < UNITS:
+                il_w_g(s + 2)
+            quant(zil, zq, s, "z")
+            if s == CELL_AT:
                 for ft in range(FT):
-                    if FC_SLOTS[ft] == (s, "A"):
-                        f_times_c(ft)
-                if s + 2 < NG and not (G_EARLY and s in QW_FIRST):
-                    il_w_gpsimd(s + 2)
-            if s + LEADW < NG and (not QZ_EARLY or s in QZ_LATE):
-                il_w(s + LEADW)
-            if s == EARLY_OUT:
-                early_out()
-            if s < NG and s not in Q_PIECES:
-                quant(zil, zq, s, "z")
-                waiting.append(s)
-            if FC_EARLY:
-                for ft in range(FT):
-                    if FC_SLOTS[ft] == (s, "B"):
-                        f_times_c(ft)
-                if CELL_SLOT == s:
-                    new_cell()
-                if s + 1 < NG:
-                    il_z_gpsimd(s + 1)
-            if s in Q_PIECES:
-                n = Q_PIECES[s]
-                w = width[s] // n
-                for k in range(n):
-                    quant(wil, wq, s, "w", k * w, (k + 1) * w)
-                    quant(zil, zq, s, "z", k * w, (k + 1) * w)
-                    mm(s, only=list(range(k * w // P, (k + 1) * w // P)))
-                    if k in WEAVE_AFTER and rg2:
-                        reduce_gate(2, rg2[0])
-                        rg2.remove(rg2[0])
-            if s + LEADW < NG and QZ_EARLY and s not in QZ_LATE:
-                il_w(s + LEADW)
-            if s == QUANT_H:
-                quant_h()
-                have_h = True
-            if have_h:
-                for g in waiting:
-                    mm(g)
-                waiting = []
-            if s == TURN_C:
-                turn_c()
-            for ft in range(FT):
-                if st[3] + FC_AFTER + ft // FC_PER_STAGE == s and not FC_EARLY:
-                    f_times_c(ft)
-            for ft in range(RG1_NOW, FT):
-                if st[7] + 1 + (ft - RG1_NOW) // RG1_PER_STAGE == s:
-                    reduce_gate(1, ft)
-            if s == st[7] + CELL_AFTER and CELL_SLOT < 0 and CELL_BEHIND_ILZ < 0:
+                    if RG1_AT[ft] == s:
+                        sum_bones(1, ft, acc[1][:, ft * P:(ft + 1) * P])
                 new_cell()
-            for ft in rg2:
-                reduce_gate(2, ft)
-            rg2.clear()
-            if s in FLUSH_AT:
-                sigs(99)
-            for k in range(LOADS_PER_STAGE):
+            il_z_g(s + 1)
+            widen_v(s + 2)
+            il_w(s + 1, 0, H if s + 1 < LAST else H // 2 if TAIL_SPLIT else H)
+            if s != CELL_AT:
+                for ft in range(FT):
+                    if RG1_AT[ft] == s:
+                        if ft == 0:
+                            acc_tile(1)
+                        sum_bones(1, ft, acc[1][:, ft * P:(ft + 1) * P])
+            if s == 1:
+                quant_h()
+                mm(0, range(FT))
+            if s >= 1:
+                mm(s, range(FT))
+            for ft in range(FT):
+                if CT_AT[ft] == s:
+                    turn_c(ft)
+            for k in range(2):
                 if later:
                     load_named(later.pop(0))
 
-        if EARLY_OUT == 99:
-            early_out()
-        for k in range(LATE - 1):
-            nc.vector.tensor_reduce(out=r3[:, :, R + k * B:R + (k + 1) * B],
-                                    in_=last[:, :, :, k, :].rearrange("p f n b -> p f b n"), axis=AX.X, op=ALU.add)
-        acc3 = aux.tile([P, H], F32, name="acc3", tag="aux")
+        nc.scalar.activation(out=s2[:], in_=cnew[:], func=ACT.Sigmoid, scale=2.0)
+        if AFFINE_ON_S:
+            nc.scalar.activation(out=s2[:], in_=s2[:], func=ACT.Copy, scale=0.25, bias=-0.125)
+        tags = ["c0", "c1", "c2"]
+        acc[2] = aux.tile([P, 2, P], F32, name="acc2", tag=tags[0])
+
+        def early(f0, f1):
+            src = acc[2] if f0 == 0 else acc[3]
+            fs = slice(f0 * P, f1 * P)
+            nc.vector.tensor_tensor(out=gnew[0:R, fs], in0=src[0:R].rearrange("p f c -> p (f c)"), in1=s2[0:R, fs], op=ALU.mult)
+
+        def late(f0, f1):
+            fs = slice(f0 * P, f1 * P)
+            nc.vector.tensor_tensor(out=gnew[R:P, fs], in0=acc[4][R:P, fs], in1=s2[R:P, fs], op=ALU.mult)
+
+        def last_sum(ft):
+            nc.vector.tensor_reduce(out=r3[:, ft, R:P], in_=last[:, ft].rearrange("p n b -> p b n"), axis=AX.X, op=ALU.add)
+
+        def last_turn(ft):
+            nc.tensor.transpose(acc[4][:, ft * P:(ft + 1) * P], r3[:, ft, :], ident_f[:])
+
+        for ft in range(EARLY_SUMS):
+            sum_bones(2, ft, acc[2][:, ft, :])
+        half = H // 2
+        if TAIL_SPLIT:
+            il_z(LAST, 0, half)
+            quant(wil, wq, LAST, "w", 0, half)
+            quant(zil, zq, LAST, "z", 0, P)
+            mm(LAST, [0])
+            quant(zil, zq, LAST, "z", P, half)
+            mm(LAST, [1])
+            il_z(LAST, half, H)
+            il_w(LAST, half, H)
+            quant(wil, wq, LAST, "w", half, H)
+            quant(zil, zq, LAST, "z", half, half + P)
+            mm(LAST, [2])
+            quant(zil, zq, LAST, "z", half + P, H)
+            mm(LAST, [3])
+        else:
+            il_z(LAST)
+            for ft in range(FT):
+                quant(wil, wq, LAST, "w", ft * P, (ft + 1) * P)
+                quant(zil, zq, LAST, "z", ft * P, (ft + 1) * P)
+                mm(LAST, [ft])
+        if not AFFINE_ON_S:
+            nc.vector.tensor_scalar(out=s2[:], in0=s2[:], scalar1=0.25, scalar2=-0.125, op0=ALU.mult, op1=ALU.add)
+        sigs(FT)
+        for ft in range(EARLY_SUMS, 2):
+            sum_bones(2, ft, acc[2][:, ft, :])
+        acc[3] = aux.tile([P, 2, P], F32, name="acc2b", tag=tags[1])
+        acc[4] = aux.tile([P, H], F32, name="acc3", tag=tags[2])
+        if EARLY_FIRST:
+            early(0, 2)
         for ft in range(FT):
-            if ft == EARLY_OUT - 100:
-                early_out()
-            nc.vector.tensor_reduce(out=r3[:, ft, P - B:P], in_=last[:, ft, :, LATE - 1, :].rearrange("p n b -> p b n"),
-                                    axis=AX.X, op=ALU.add)
-            nc.tensor.transpose(acc3[:, ft * P:(ft + 1) * P], r3[:, ft, :], ident_f[:])
-            if ft == FT - 1 and EARLY_OUT == 104:
-                early_out()
-            if (ft + 1) % END_STEP == 0:
-                fs = slice((ft + 1 - END_STEP) * P, (ft + 1) * P)
-                nc.vector.tensor_tensor(out=gnew[R:P, fs], in0=acc3[R:P, fs], in1=s2[R:P, fs], op=ALU.mult)
-        for t in range(T - LATE, T):
+            last_sum(ft)
+        for ft in (2, 3):
+            sum_bones(2, ft, acc[3][:, ft - 2, :])
+        for ft in range(FT):
+            last_turn(ft)
+        if not EARLY_FIRST:
+            early(0, 2)
+        early(2, 4)
+        for t in range(T - 1):
             nc.sync.dma_start(out=out_0[:, t, :], in_=gnew[t * B:(t + 1) * B, :])
+        for f0 in range(0, FT, LATE_STEP):
+            late(f0, f0 + LATE_STEP)
+        nc.sync.dma_start(out=out_0[:, T - 1, :], in_=gnew[R:P, :])

from contextlib import ExitStack

import concourse.mybir as mybir
from concourse.masks import make_identity

F32 = mybir.dt.float32
BF16 = mybir.dt.bfloat16
I32 = mybir.dt.int32
U32 = mybir.dt.uint32
U8 = mybir.dt.uint8
FP8 = mybir.dt.float8_e4m3fn
FP8X4 = mybir.dt.float8_e4m3fn_x4
ACT = mybir.ActivationFunctionType
ALU = mybir.AluOpType
AX = mybir.AxisListType

P = 128
B, T, NB, H, GH = 32, 4, 8, 512, 3
FT = H // P
UNITS = GH * T
COLS = NB * B
LAST = UNITS - 1

PIN_PE = True
LOADS = ["zscale", "z0.0", "w0.0", "z0.1", "w0.1", "z0.2", "w0.2", "z0.3", "w0.3", "z1", "w1", "z2", "h", "gs", "bias", "w2", "z3", "w3", "z4", "z5", "c", "w4", "w5"]
LATER = ["z6", "z7", "w6", "w7", "z8", "z9", "w8", "w9", "z10", "z11", "cgs", "w10", "w11"]
ZGROUPS = [[0], [1], [2], [3], [4, 5], [6, 7], [8, 9], [10, 11]]
W_PE = [0, 0, 0, 0, 0, 0, 0, 0, 0, 0, 0, 0]
W_S = [0, 0, 0, 0, 0, 0, 160, 96, 64, 128, 128, 192]
W_G = [0, 0, 0, 0, 0, 0, 0, 152, 152, 152, 152, 0]
Z_G = [0, 0, 0, 0, 0, 0, 0, 0, 0, 0, 0, 152]
Z_ON_V = {}
IL_FIRST = []
FC_AT = [5, 6, 7, 8]
CT_AT = [2, 2, 2, 6]
RG1_AT = [9, 9, 10, 10]
CELL_AT = 10
QW0_FIRST = False
G_FIRST = True
CELL_PARTS = 2
MX_BANKS = 4
CT_BANKS = 3
LATE_STEP = 4
EARLY_SUMS = 2
EARLY_FIRST = True
AFFINE_ON_S = True
TAIL_SPLIT = False
FLOPS = 2 * (B * NB + B) * H * H * GH * T


def tile_st_hmr_pc_kernel(tc, h_new, c_new, g_s, c_g_s, Wg_s, Zg_s_bytes, Zg_s_scale, bg_s, out_0, out_1):
    nc = tc.nc
    with ExitStack() as ctx:
        const = ctx.enter_context(tc.tile_pool(name="const", bufs=1))
        raw = ctx.enter_context(tc.tile_pool(name="raw", bufs=6))
        wide = ctx.enter_context(tc.tile_pool(name="wide", bufs=4))
        wpool = ctx.enter_context(tc.tile_pool(name="wpool", bufs=2))
        zpool = ctx.enter_context(tc.tile_pool(name="zpool", bufs=1))
        codes = ctx.enter_context(tc.tile_pool(name="codes", bufs=4))
        mxps = ctx.enter_context(tc.psum_pool(name="mxps", bufs=MX_BANKS))
        aux = ctx.enter_context(tc.psum_pool(name="aux", bufs=1))
        if PIN_PE:
            ctx.enter_context(tc.manual_schedule())
        else:
            ET = mybir.EngineType
            ctx.enter_context(tc.manual_schedule(engines={ET.DVE, ET.Activation, ET.Pool, ET.SP}))

        warm = const.tile([P, 1], F32, name="warm")
        nc.vector.memset(warm[:], 0.0)
        nc.scalar.activation(out=warm[:], in_=warm[:], func=ACT.Sigmoid)
        ident_f = const.tile([P, P], F32, name="ident_f")
        make_identity(nc, ident_f[:])
        ident_b = const.tile([P, P], BF16, name="ident_b")
        make_identity(nc, ident_b[:])
        bias_raw = const.tile([P, P], BF16, name="bias_raw")
        nc.gpsimd.memset(bias_raw[:], 0.0)
        r3 = const.tile([P, FT, P], F32, name="r3")
        nc.gpsimd.memset(r3[:], 0.0)
        gs0 = const.tile([P, T * B], U8, name="gs0", align_bytes=64)
        nc.vector.memset(gs0[:].bitcast(I32), 0)

        zscale = const.tile([P, 4], F32, name="zscale")
        h_sb = const.tile([P, NB, H], BF16, name="h_sb")
        c_sb = const.tile([P, NB, H], BF16, name="c_sb")
        gs_sb = const.tile([P, H], BF16, name="gs_sb")
        cgs = const.tile([P, H], BF16, name="cgs")
        bias_sb = const.tile([P, UNITS * FT], F32, name="bias_sb")
        hin = const.tile([P, T * COLS * 4], BF16, name="hin", align_bytes=64)
        gin0 = const.tile([P, T * B * 4], BF16, name="gin0", align_bytes=64)
        hq = const.tile([P, T * COLS], U32, name="hq", align_bytes=64)
        hs = const.tile([P, T * COLS], U8, name="hs", align_bytes=64)
        gq0 = const.tile([P, T * B], U32, name="gq0", align_bytes=64)
        gq = const.tile([P, T * COLS], U32, name="gq", align_bytes=64)
        gsc = const.tile([P, T * COLS], U8, name="gsc", align_bytes=64)
        t1 = const.tile([P, H], F32, name="t1")
        cnew = const.tile([P, H], F32, name="cnew")
        s2 = const.tile([P, H], F32, name="s2")
        gnew = const.tile([P, H], F32, name="gnew")
        gate_a = {}
        gate_b = {}
        for ft in range(FT):
            gate_a[ft] = const.tile([P, NB, T, B], F32, name="gate_a%d" % ft)
            gate_b[ft] = const.tile([P, NB, T, B], F32, name="gate_b%d" % ft)
        last = const.tile([P, FT, NB, B], F32, name="last")

        zbytes = {}
        wraw = {}
        zwide = {}
        wil = {}
        zil = {}
        wq = {}
        zq = {}
        mxp = {}
        cT = {}
        acc = {}
        pe_il = {}
        small = {}
        zg_of = {}
        for k in range(len(ZGROUPS)):
            for i in range(len(ZGROUPS[k])):
                zg_of[ZGROUPS[k][i]] = (k, i * H)

        def z_src(u):
            return Zg_s_bytes[u // T, u % T].rearrange("(p j) n -> p j n", j=4)

        def w_src(u):
            return Wg_s[u // T, u % T].rearrange("(p j) n -> p j n", j=4)

        def load_named(what):
            part = None
            if "." in what:
                what, part = what.split(".")
            if what == "zscale":
                nc.sync.dma_start(out=zscale[:], in_=Zg_s_scale[0, 0].rearrange("(p j) c -> p (j c)", j=4))
            elif what == "h":
                nc.sync.dma_start(out=h_sb[:], in_=h_new.rearrange("b t n h -> (b t) n h"))
            elif what == "gs":
                nc.sync.dma_start(out=gs_sb[:], in_=g_s.rearrange("b t h -> (b t) h"))
            elif what == "bias":
                rows = bg_s.rearrange("g t o (c f) -> (g t o c) f", f=P)
                nc.sync.dma_start(out=bias_raw[0:32, :], in_=rows[0:32])
                nc.sync.dma_start(out=bias_raw[32:48, :], in_=rows[32:48])
            elif what == "c":
                nc.sync.dma_start(out=c_sb[:], in_=c_new.rearrange("b t n h -> (b t) n h"))
            elif what == "cgs":
                for t in range(T):
                    nc.sync.dma_start(out=cgs[t * B:(t + 1) * B, :], in_=c_g_s[:, t, :])
            elif what[0] == "w":
                u = int(what[1:])
                if u not in wraw:
                    wraw[u] = raw.tile([P, 4, H], BF16, name="wraw", tag="wraw")
                cs = slice(0, H) if part is None else slice(int(part) * P, (int(part) + 1) * P)
                nc.sync.dma_start(out=wraw[u][:, :, cs], in_=w_src(u)[:, :, cs])
            else:
                u = int(what[1:])
                k, o = zg_of[u]
                if k not in zbytes:
                    zbytes[k] = raw.tile([P, 4, H * len(ZGROUPS[k])], U8, name="zbytes", tag="zbytes")
                if part is None:
                    nc.sync.dma_start(out=zbytes[k][:, :, o:o + H], in_=z_src(u))
                else:
                    nc.sync.dma_start(out=zbytes[k][:, int(part), o:o + H], in_=z_src(u)[:, int(part)])

        def widen(u):
            k, o = zg_of[u]
            if k in zwide:
                return
            zwide[k] = wide.tile([P, 4, H * len(ZGROUPS[k])], BF16, name="zwide", tag="zwide")
            for j in range(4):
                if k in Z_ON_V and j in Z_ON_V[k]:
                    continue
                nc.scalar.activation(out=zwide[k][:, j, :], in_=zbytes[k][:, j, :].bitcast(FP8), func=ACT.Copy, scale=zscale[:, j:j + 1])

        def widen_v(u):
            k, o = zg_of.get(u, (0, 1))
            if o == 0 and k in Z_ON_V:
                for j in Z_ON_V[k]:
                    nc.vector.tensor_scalar(out=zwide[k][:, j, :], in0=zbytes[k][:, j, :].bitcast(FP8), scalar1=zscale[:, j:j + 1],
                                            scalar2=None, op0=ALU.mult)

        def runs(ap):
            return ap.rearrange("p (g i) j -> p g j i", i=4)

        def rows(ap):
            return ap.rearrange("p j (g i) -> p g j i", i=4)

        def wil_of(u):
            if u not in wil:
                wil[u] = wpool.tile([P, H, 4], BF16, name="wil", tag="wil", align_bytes=64)
            return wil[u]

        def zil_of(u):
            if u not in zil:
                zil[u] = zpool.tile([P, H, 4], BF16, name="zil", tag="zil", align_bytes=64)
            return zil[u]

        def zw(u, a, b):
            k, o = zg_of[u]
            return zwide[k][:, :, o + a:o + b]

        def il_w_pe(u):
            n = W_PE[u]
            if n:
                pe_il[u] = aux.tile([P, n, 4], BF16, name="pe_il", tag="il")
                for a in range(0, n, P):
                    nc.tensor.matmul(out=pe_il[u][:, a:a + P, :], lhsT=ident_b[:],
                                     rhs=wraw[u][:, :, H - n + a:H - n + a + P].rearrange("p j c -> p c j"), start=True, stop=True)

        def il_w_s(u):
            e = H - W_PE[u]
            if W_PE[u]:
                nc.scalar.copy(out=wil_of(u)[:, e:H, :], in_=pe_il[u][:])
            if W_S[u]:
                a = e - W_S[u]
                nc.scalar.copy(out=runs(wil_of(u)[:, a:e, :]), in_=rows(wraw[u][:, :, a:e]))

        def il_w_g(u):
            e = H - W_PE[u] - W_S[u]
            if W_G[u]:
                a = e - W_G[u]
                nc.gpsimd.tensor_scalar(out=runs(wil_of(u)[:, a:e, :]), in0=rows(wraw[u][:, :, a:e]), scalar1=1.0, scalar2=0.0,
                                        op0=ALU.mult, op1=ALU.add)

        def il_w(u, a=0, b=H):
            b = min(b, H - W_PE[u] - W_S[u] - W_G[u])
            if a < b:
                nc.vector.tensor_copy(out=runs(wil_of(u)[:, a:b, :]), in_=rows(wraw[u][:, :, a:b]))

        def il_z_g(u):
            if Z_G[u]:
                a = H - Z_G[u]
                nc.gpsimd.tensor_scalar(out=runs(zil_of(u)[:, a:H, :]), in0=rows(zw(u, a, H)), scalar1=1.0, scalar2=0.0,
                                        op0=ALU.mult, op1=ALU.add)

        def il_z(u, a=0, b=H):
            b = min(b, H - Z_G[u])
            if a < b:
                nc.vector.tensor_copy(out=runs(zil_of(u)[:, a:b, :]), in_=rows(zw(u, a, b)))

        def quant(src, store, u, nm, a=0, b=H):
            if u not in store:
                store[u] = (codes.tile([P, H], U32, name=nm + "q", tag=nm + "q", align_bytes=64),
                            codes.tile([P, H], U8, name=nm + "s", tag=nm + "s", align_bytes=64))
            q, s = store[u]
            nc.vector.quantize_mx(out=q[:, a:b].bitcast(FP8X4), scales=s[:, a:b], in_=src[u][:, a:b, :].rearrange("p c j -> p (c j)"))

        pend = []

        def mm(u, fts):
            t = u % T
            cols = slice(t * COLS, (t + 1) * COLS)
            for ft in fts:
                if u == LAST:
                    mxp[(u, ft)] = mxps.tile([P, COLS], F32, name="mxp", tag="mxp")
                    ps = mxp[(u, ft)][:]
                else:
                    if ft % 2 == 0:
                        mxp[(u, ft // 2)] = mxps.tile([P, 2, COLS], F32, name="mxp", tag="mxp")
                    ps = mxp[(u, ft // 2)][:, ft % 2, :]
                fs = slice(ft * P, (ft + 1) * P)
                nc.tensor.matmul_mx(out=ps, lhsT=wq[u][0][:, fs].bitcast(FP8X4), lhsT_scale=wq[u][1][:, fs],
                                    rhs=hq[:, cols].bitcast(FP8X4), rhs_scale=hs[:, cols], start=True, stop=False)
                nc.tensor.matmul_mx(out=ps, lhsT=zq[u][0][:, fs].bitcast(FP8X4), lhsT_scale=zq[u][1][:, fs],
                                    rhs=gq[:, cols].bitcast(FP8X4), rhs_scale=gsc[:, cols], start=False, stop=True)
                pend.append((u, ft))

        def sigs(n):
            for k in range(min(n, len(pend))):
                u, ft = pend.pop(0)
                g, t = u // T, u % T
                if u == LAST:
                    dst, ps = last[:, ft], mxp[(u, ft)][:]
                else:
                    dst, ps = (gate_b if g == 1 else gate_a)[ft][:, :, t, :], mxp[(u, ft // 2)][:, ft % 2, :]
                nc.scalar.activation(out=dst, in_=ps.rearrange("p (n b) -> p n b", b=B), func=ACT.Sigmoid,
                                     bias=bias_sb[:, u * FT + ft:u * FT + ft + 1], scale=1.0)

        def sum_bones(g, ft, dst):
            src = gate_b[ft] if g == 1 else gate_a[ft]
            for n in range(NB):
                nc.tensor.matmul(out=dst, lhsT=src[:, n].rearrange("p t b -> p (t b)"), rhs=ident_f[:], is_transpose=True,
                                 start=(n == 0), stop=(n == NB - 1))

        hin_w = hin[:].bitcast(F32).rearrange("p (t n b u) -> p t n b u", t=T, n=NB, b=B, u=2)

        def turn_h():
            hw = h_sb[:].bitcast(F32)
            tags = [(mxps, "mxp"), (aux, "c0"), (mxps, "mxp"), (aux, "c1"), (mxps, "mxp"), (aux, "c2"), (mxps, "mxp"), (aux, "c3")]
            if CT_BANKS < 4:
                tags[7] = (aux, "il")
            hTs = []
            for n in range(NB):
                pool, tag = tags[n]
                hT = pool.tile([P, 2, P], F32, name="hT", tag=tag)
                for u in range(2):
                    nc.tensor.transpose(hT[:, u, :], hw[:, n, u::2], ident_f[:])
                hTs.append(hT)
                nc.scalar.copy(out=hin_w[:, :, n, :, :], in_=hT[:].rearrange("p u (b t) -> p t b u", t=T))
            gw = gs_sb[:].bitcast(F32)
            gT = mxps.tile([P, 2, P], F32, name="gT", tag="mxp")
            for u in range(2):
                nc.tensor.transpose(gT[:, u, :], gw[:, u::2], ident_f[:])
            small["bT"] = mxps.tile([P, P], BF16, name="bT", tag="mxp")
            nc.tensor.transpose(small["bT"][:], bias_raw[:], ident_b[:])
            nc.scalar.copy(out=gin0[:].bitcast(F32).rearrange("p (t b u) -> p t b u", t=T, b=B, u=2),
                           in_=gT[:].rearrange("p u (b t) -> p t b u", t=T))

        def quant_h():
            if G_FIRST:
                nc.vector.quantize_mx(out=gq0[:].bitcast(FP8X4), scales=gs0[:], in_=gin0[:])
                nc.vector.quantize_mx(out=hq[:].bitcast(FP8X4), scales=hs[:], in_=hin[:])
            else:
                nc.vector.tensor_copy(out=bias_sb[:], in_=small["bT"][:, 0:UNITS * FT])
                nc.vector.quantize_mx(out=hq[:].bitcast(FP8X4), scales=hs[:], in_=hin[:])
                nc.vector.quantize_mx(out=gq0[:].bitcast(FP8X4), scales=gs0[:], in_=gin0[:])
            nc.vector.tensor_copy(
                out=gq[:].bitcast(I32).rearrange("p (t n b) -> p t n b", t=T, n=NB, b=B),
                in_=gq0[:].bitcast(I32).rearrange("p (t b) -> p t b", t=T).unsqueeze(2).to_broadcast([P, T, NB, B]))
            nc.vector.tensor_copy(
                out=gsc[:].bitcast(I32).rearrange("p (t n w) -> p t n w", t=T, n=NB, w=B // 4),
                in_=gs0[:].bitcast(I32).rearrange("p (t w) -> p t w", t=T).unsqueeze(2).to_broadcast([P, T, NB, B // 4]))
            if G_FIRST:
                nc.vector.tensor_copy(out=bias_sb[:], in_=small["bT"][:, 0:UNITS * FT])

        def turn_c(ft):
            cT[ft] = aux.tile([P, NB, P], BF16, name="cT", tag="c%d" % (ft if ft < CT_BANKS else 1))
            for n in range(NB):
                nc.tensor.transpose(cT[ft][:, n, :], c_sb[:, n, ft * P:(ft + 1) * P], ident_b[:])

        def acc_tile(g):
            tags = ["c0", "c2"]
            acc[g] = aux.tile([P, H], F32, name="acc", tag=tags[g])

        def f_times_c(ft):
            f = gate_a[ft]
            nc.vector.tensor_tensor(out=f[:], in0=f[:], in1=cT[ft][:].rearrange("p n (b t) -> p n t b", t=T), op=ALU.mult)

        def new_cell():
            for c in range(0, H, H // CELL_PARTS):
                cs = slice(c, c + H // CELL_PARTS)
                nc.vector.scalar_tensor_tensor(out=t1[:, cs], in0=acc[1][:, cs], scalar=0.125, in1=cgs[:, cs], op0=ALU.mult, op1=ALU.mult)
            for c in range(0, H, H // CELL_PARTS):
                cs = slice(c, c + H // CELL_PARTS)
                nc.vector.scalar_tensor_tensor(out=cnew[:, cs], in0=acc[0][:, cs], scalar=0.125, in1=t1[:, cs], op0=ALU.mult, op1=ALU.add)
            for t in range(T):
                nc.sync.dma_start(out=out_1[:, t, :], in_=cnew[t * B:(t + 1) * B, :])

        R = (T - 1) * B

        for what in LOADS:
            load_named(what)
        later = list(LATER)
        for u in range(3):
            widen(u)
        for c in range(FT):
            il_w(0, c * P, (c + 1) * P)

        for s in range(UNITS):
            if s == 0:
                turn_h()
            if s + 2 < UNITS and s not in IL_FIRST:
                widen(s + 2)
            if s + 1 < UNITS:
                il_w_s(s + 1)
            if s + 2 < UNITS and s in IL_FIRST:
                widen(s + 2)
            if s + 2 < UNITS:
                il_w_pe(s + 2)
            sigs(8)
            if s == LAST:
                break
            if s == 0 and QW0_FIRST:
                quant(wil, wq, s, "w")
                il_z(s)
            else:
                il_z(s)
                quant(wil, wq, s, "w")
            if s in FC_AT:
                ft = FC_AT.index(s)
                f_times_c(ft)
                if ft == 0:
                    acc_tile(0)
                sum_bones(0, ft, acc[0][:, ft * P:(ft + 1) * P])
            if s + 2 < UNITS:
                il_w_g(s + 2)
            quant(zil, zq, s, "z")
            if s == CELL_AT:
                for ft in range(FT):
                    if RG1_AT[ft] == s:
                        sum_bones(1, ft, acc[1][:, ft * P:(ft + 1) * P])
                new_cell()
            il_z_g(s + 1)
            widen_v(s + 2)
            il_w(s + 1, 0, H if s + 1 < LAST else H // 2 if TAIL_SPLIT else H)
            if s != CELL_AT:
                for ft in range(FT):
                    if RG1_AT[ft] == s:
                        if ft == 0:
                            acc_tile(1)
                        sum_bones(1, ft, acc[1][:, ft * P:(ft + 1) * P])
            if s == 1:
                quant_h()
                mm(0, range(FT))
            if s >= 1:
                mm(s, range(FT))
            for ft in range(FT):
                if CT_AT[ft] == s:
                    turn_c(ft)
            for k in range(2):
                if later:
                    load_named(later.pop(0))

        nc.scalar.activation(out=s2[:], in_=cnew[:], func=ACT.Sigmoid, scale=2.0)
        if AFFINE_ON_S:
            nc.scalar.activation(out=s2[:], in_=s2[:], func=ACT.Copy, scale=0.25, bias=-0.125)
        tags = ["c0", "c1", "c2"]
        acc[2] = aux.tile([P, 2, P], F32, name="acc2", tag=tags[0])

        def early(f0, f1):
            src = acc[2] if f0 == 0 else acc[3]
            fs = slice(f0 * P, f1 * P)
            nc.vector.tensor_tensor(out=gnew[0:R, fs], in0=src[0:R].rearrange("p f c -> p (f c)"), in1=s2[0:R, fs], op=ALU.mult)

        def late(f0, f1):
            fs = slice(f0 * P, f1 * P)
            nc.vector.tensor_tensor(out=gnew[R:P, fs], in0=acc[4][R:P, fs], in1=s2[R:P, fs], op=ALU.mult)

        def last_sum(ft):
            nc.vector.tensor_reduce(out=r3[:, ft, R:P], in_=last[:, ft].rearrange("p n b -> p b n"), axis=AX.X, op=ALU.add)

        def last_turn(ft):
            nc.tensor.transpose(acc[4][:, ft * P:(ft + 1) * P], r3[:, ft, :], ident_f[:])

        for ft in range(EARLY_SUMS):
            sum_bones(2, ft, acc[2][:, ft, :])
        half = H // 2
        if TAIL_SPLIT:
            il_z(LAST, 0, half)
            quant(wil, wq, LAST, "w", 0, half)
            quant(zil, zq, LAST, "z", 0, P)
            mm(LAST, [0])
            quant(zil, zq, LAST, "z", P, half)
            mm(LAST, [1])
            il_z(LAST, half, H)
            il_w(LAST, half, H)
            quant(wil, wq, LAST, "w", half, H)
            quant(zil, zq, LAST, "z", half, half + P)
            mm(LAST, [2])
            quant(zil, zq, LAST, "z", half + P, H)
            mm(LAST, [3])
        else:
            il_z(LAST)
            for ft in range(FT):
                quant(wil, wq, LAST, "w", ft * P, (ft + 1) * P)
                quant(zil, zq, LAST, "z", ft * P, (ft + 1) * P)
                mm(LAST, [ft])
        if not AFFINE_ON_S:
            nc.vector.tensor_scalar(out=s2[:], in0=s2[:], scalar1=0.25, scalar2=-0.125, op0=ALU.mult, op1=ALU.add)
        sigs(FT)
        for ft in range(EARLY_SUMS, 2):
            sum_bones(2, ft, acc[2][:, ft, :])
        acc[3] = aux.tile([P, 2, P], F32, name="acc2b", tag=tags[1])
        acc[4] = aux.tile([P, H], F32, name="acc3", tag=tags[2])
        if EARLY_FIRST:
            early(0, 2)
        for ft in range(FT):
            last_sum(ft)
        for ft in (2, 3):
            sum_bones(2, ft, acc[3][:, ft - 2, :])
        for ft in range(FT):
            last_turn(ft)
        if not EARLY_FIRST:
            early(0, 2)
        early(2, 4)
        for t in range(T - 1):
            nc.sync.dma_start(out=out_0[:, t, :], in_=gnew[t * B:(t + 1) * B, :])
        for f0 in range(0, FT, LATE_STEP):
            late(f0, f0 + LATE_STEP)
        nc.sync.dma_start(out=out_0[:, T - 1, :], in_=gnew[R:P, :])
